import numpy as np
import ml_dtypes


def mxq(x, axis, fmt="e4m3"):
    dtype, down = {"e4m3": (ml_dtypes.float8_e4m3fn, 7), "e5m2": (ml_dtypes.float8_e5m2, 14)}[fmt]
    v = np.moveaxis(np.asarray(x, np.float32).astype(ml_dtypes.bfloat16).astype(np.float64), axis, -1)
    blocks = v.reshape(v.shape[:-1] + (-1, 32))
    amax = np.abs(blocks).max(-1, keepdims=True)
    byte = np.maximum(np.where(amax > 0, np.frexp(amax)[1] - 1 + 127, 0) - down, 1)
    scale = np.exp2(byte - 127.0)
    codes = (blocks / scale).astype(np.float32).astype(dtype).astype(np.float64)
    return np.moveaxis((codes * scale).reshape(v.shape), -1, axis)


WIDE = False


def mx_kscale(k):
    if not WIDE:
        return np.ones(k)
    levels = np.array([10, -10, 5, -5, 0])
    a = np.random.permutation(np.resize(levels, k // 512 * 4)).reshape(k // 512, 4)
    idx = np.arange(k)
    return np.exp2(a[idx // 512, idx % 128 // 32])


BF16 = ml_dtypes.bfloat16


def bf(x):
    return np.asarray(x, np.float32).astype(BF16)


def f64(x):
    return np.asarray(x).astype(np.float64)


B, G, C, D, E, S = 2, 4, 512, 1024, 1024, 128
N = G * C


def setup_inputs():
    s = mx_kscale(D)
    return {"x": bf(np.random.standard_normal((B, N, D)) * s),
            "Wve": bf(np.random.standard_normal((D, E)) / np.sqrt(D) / s[:, None]),
            "bve": bf(np.random.standard_normal(E) * 0.1),
            "Wxs": bf(np.random.standard_normal((D, S)) / np.sqrt(D) / s[:, None]),
            "bxs": bf(np.random.standard_normal(S) * 0.1),
            "gamma_k_lin": bf(np.random.standard_normal(S) * 0.2),
            "beta_k_lin": bf(np.random.standard_normal(S) * 0.05)}


def reference(x, Wve, bve, Wxs, bxs, gamma_k_lin, beta_k_lin):
    xq = mxq(f64(x), 2, "e4m3")
    v = np.tanh((xq @ mxq(f64(Wve), 0, "e4m3")) + f64(bve))
    z = np.tanh((xq @ mxq(f64(Wxs), 0, "e4m3")) + f64(bxs))
    k_lin = z * f64(gamma_k_lin) + f64(beta_k_lin)
    return mxq(k_lin, 1, "e4m3").transpose(0, 2, 1) @ mxq(v, 1, "e4m3")

@@ -1,0 +1,331 @@
+from contextlib import ExitStack
+
+import concourse.mybir as mybir
+from concourse.masks import make_identity
+
+F32 = mybir.dt.float32
+BF16 = mybir.dt.bfloat16
+U32 = mybir.dt.uint32
+U8 = mybir.dt.uint8
+FP8X4 = mybir.dt.float8_e4m3fn_x4
+ACT = mybir.ActivationFunctionType
+ALU = mybir.AluOpType
+
+P = 128
+B, NTOK, D, E, S = 2, 2048, 1024, 1024, 128
+GROUP = 512
+NG = B * NTOK // GROUP
+GPB = NTOK // GROUP
+EQ = 256
+NQ = E // EQ
+
+FLOPS = 2 * B * NTOK * D * (E + S) + 2 * B * NTOK * S * E
+
+PIN = True
+
+
+def tile_flashattention_pb_t_kernel(tc, x, Wve, bve, Wxs, bxs, gamma_k_lin, beta_k_lin, out):
+    nc = tc.nc
+    with ExitStack() as ctx:
+        if PIN:
+            ctx.enter_context(tc.manual_schedule())
+        const = ctx.enter_context(tc.tile_pool(name="const", bufs=1))
+        xin = ctx.enter_context(tc.tile_pool(name="xin", bufs=4))
+        work = ctx.enter_context(tc.tile_pool(name="work", bufs=2))
+        psum = ctx.enter_context(tc.psum_pool(name="psum", bufs=1))
+
+        xv = x.rearrange("b (g p j) d -> (b g) p (j d)", g=GPB, p=P, j=4)
+        xs = {}
+
+        def load_x(g, pieces=1):
+            t = xin.tile([P, 4 * D], BF16, name="xs", tag="xs")
+            w = 4 * D // pieces
+            for i in range(pieces):
+                nc.sync.dma_start(out=t[:, i * w : (i + 1) * w], in_=xv[g][:, i * w : (i + 1) * w])
+            xs[g] = t
+
+        warm = const.tile([P, 1], F32, name="warm")
+        warm2 = const.tile([P, 1], F32, name="warm2")
+        rows = const.tile([P, E], BF16, name="rows")
+        small = const.tile([P, P], BF16, name="small")
+        ones_b = const.tile([P, P], BF16, name="ones_b")
+        nc.vector.memset(rows[:], 0.0)
+        nc.vector.memset(small[:], 0.0)
+        nc.vector.memset(warm[:], 0.0)
+        nc.vector.memset(ones_b[:], 1.0)
+        nc.scalar.activation(out=warm2[:], in_=warm[:], func=ACT.Tanh)
+        load_x(0, pieces=2)
+        nc.sync.dma_start(out=rows[0:1, :], in_=bve.unsqueeze(0))
+        nc.sync.dma_start(out=small[0:1, :], in_=bxs.unsqueeze(0))
+        nc.sync.dma_start(out=small[1:2, :], in_=gamma_k_lin.unsqueeze(0))
+        nc.sync.dma_start(out=small[2:3, :], in_=beta_k_lin.unsqueeze(0))
+
+        wraw = const.tile([P, 2, 4, E], BF16, name="wraw")
+        wview = Wve.rearrange("(c u p e) n -> c p u (e n)", c=2, u=2, p=P, e=2)
+        for c in range(2):
+            nc.sync.dma_start(out=wraw[:, c, :, :].rearrange("p (u e) n -> p u (e n)", u=2), in_=wview[c])
+        wxraw = const.tile([P, 2, 4, S], BF16, name="wxraw")
+        nc.sync.dma_start(
+            out=wxraw[:].rearrange("p c (u e) n -> p (c u) (e n)", u=2),
+            in_=Wxs.rearrange("(a p e) n -> p a (e n)", a=4, p=P, e=2),
+        )
+        for g in range(1, 4):
+            load_x(g)
+
+        ident_f = const.tile([P, P], F32, name="ident_f")
+        make_identity(nc, ident_f[:])
+        ident_b = const.tile([P, P], BF16, name="ident_b")
+        make_identity(nc, ident_b[:])
+
+        wg = const.tile([P, NQ, 2, EQ, 4], BF16, name="wg", align_bytes=64)
+        wq = const.tile([P, NQ, 2, EQ], U32, name="wq", align_bytes=64)
+        wsc = const.tile([P, NQ, 2, EQ], U8, name="wsc", align_bytes=64)
+        wxg = const.tile([P, 2, S, 4], BF16, name="wxg", align_bytes=64)
+        wxq = const.tile([P, 2, S], U32, name="wxq", align_bytes=64)
+        wxsc = const.tile([P, 2, S], U8, name="wxsc", align_bytes=64)
+
+        def regroup(eng_copy, dst, src):
+            eng_copy(
+                out=dst.rearrange("p (n i) t -> p n t i", i=4),
+                in_=src.rearrange("p t (n i) -> p n t i", i=4),
+            )
+
+        def regroup_w(eng_copy, q, c):
+            regroup(eng_copy, wg[:, q, c, :, :], wraw[:, c, :, q * EQ : (q + 1) * EQ])
+
+        def quant_w(q):
+            nc.vector.quantize_mx(
+                out=wq[:, q, :, :].rearrange("p c n -> p (c n)").bitcast(FP8X4),
+                scales=wsc[:, q, :, :].rearrange("p c n -> p (c n)"),
+                in_=wg[:, q, :, :, :].rearrange("p c n t -> p (c n t)"),
+            )
+
+        gxs, xqs, xscs = {}, {}, {}
+
+        def transposes(g, copy_engines):
+            xw = xs[g][:].bitcast(F32)
+            gx = work.tile([P, 4 * D], BF16, name="gx", tag="gx", align_bytes=64)
+            gxs[g] = gx
+            gxw = gx[:].bitcast(F32).rearrange("p (a c b t u) -> p a c b t u", a=2, c=2, b=2, t=P, u=2)
+            for j in range(4):
+                xt = psum.tile([P, 4, P], F32, name="xt", tag="xt", bufs=4)
+                for a in range(4):
+                    col = j * 512 + a * P
+                    nc.tensor.transpose(xt[:, a, :], xw[:, col : col + P], ident_f[:])
+                copy_engines[j](
+                    out=gxw[:, j // 2, :, j % 2, :, :],
+                    in_=xt[:].rearrange("p (c u) t -> p c t u", u=2),
+                )
+            if g + 4 < NG:
+                load_x(g + 4)
+
+        def alloc_xq(g):
+            xqs[g] = work.tile([P, 2 * GROUP], U32, name="xq", tag="xq", align_bytes=64)
+            xscs[g] = work.tile([P, 2 * GROUP], U8, name="xsc", tag="xsc", align_bytes=64)
+
+        def quant_x(g, lo, hi):
+            nc.vector.quantize_mx(
+                out=xqs[g][:, lo:hi].bitcast(FP8X4), scales=xscs[g][:, lo:hi], in_=gxs[g][:, 4 * lo : 4 * hi]
+            )
+
+        s_copy = nc.scalar.copy
+        v_copy = nc.vector.tensor_copy
+        transposes(0, [s_copy, v_copy, s_copy, v_copy])
+        alloc_xq(0)
+        quant_x(0, 0, GROUP)
+        quant_x(0, GROUP, 2 * GROUP)
+
+        bias = const.tile([P, E], F32, name="bias")
+        for h in range(2):
+            pb = psum.tile([P, 512], F32, name="pb", tag="vb", bufs=3)
+            nc.tensor.matmul(out=pb[:], lhsT=ones_b[:], rhs=rows[:, h * 512 : (h + 1) * 512], start=True, stop=True)
+            nc.scalar.copy(out=bias[:, h * 512 : (h + 1) * 512], in_=pb[:])
+        sp = psum.tile([P, P], BF16, name="sp", tag="zk", bufs=1)
+        nc.tensor.transpose(sp[:], small[:], ident_b[:])
+        pvec = const.tile([P, 4], F32, name="pvec")
+        nc.vector.tensor_copy(out=pvec[:, 0:3], in_=sp[:, 0:3])
+
+        regroup_w(v_copy, 0, 0)
+        regroup_w(s_copy, 2, 0)
+        regroup_w(v_copy, 1, 0)
+        regroup_w(s_copy, 3, 0)
+        regroup_w(v_copy, 0, 1)
+        regroup_w(s_copy, 2, 1)
+        quant_w(0)
+        regroup_w(v_copy, 1, 1)
+        regroup_w(s_copy, 3, 1)
+        quant_w(1)
+        for c in range(2):
+            regroup(s_copy, wxg[:, c, :, :], wxraw[:, c, :, :])
+
+        gvs, vqs, vscs, zts, kTs, gks, kqs, kscs, us = {}, {}, {}, {}, {}, {}, {}, {}, {}
+
+        def v_passes_adds(g, q):
+            u = work.tile([P, 2, EQ, 2], F32, name="u", tag="u", bufs=4)
+            us[(g, q)] = u
+            for jj in range(2):
+                vb = psum.tile([P, 2, EQ], F32, name="vb", tag="vb", bufs=3)
+                for j2 in range(2):
+                    for c in range(2):
+                        col = jj * GROUP + c * 256 + j2 * P
+                        nc.tensor.matmul_mx(
+                            out=vb[:, j2, :],
+                            lhsT=xqs[g][:, col : col + P].bitcast(FP8X4),
+                            lhsT_scale=xscs[g][:, col : col + P],
+                            rhs=wq[:, q, c, :].bitcast(FP8X4),
+                            rhs_scale=wsc[:, q, c, :],
+                            start=(c == 0),
+                            stop=(c == 1),
+                        )
+                nc.vector.tensor_tensor(
+                    out=u[:, jj, :, :],
+                    in0=vb[:].rearrange("p b e -> p e b"),
+                    in1=bias[:, q * EQ : (q + 1) * EQ].unsqueeze(2).to_broadcast([P, EQ, 2]),
+                    op=ALU.add,
+                )
+
+        def tanh_v(g, q):
+            nc.scalar.activation(
+                out=gvs[g][:, q * EQ : (q + 1) * EQ, :].rearrange("p e (a b) -> p e a b", a=2),
+                in_=us[(g, q)][:].rearrange("p a e b -> p e a b"),
+                func=ACT.Tanh,
+            )
+
+        def quant_v(g, lo, hi):
+            nc.vector.quantize_mx(
+                out=vqs[g][:, lo:hi].bitcast(FP8X4),
+                scales=vscs[g][:, lo:hi],
+                in_=gvs[g][:, lo:hi, :].rearrange("p e j -> p (e j)"),
+            )
+
+        def z_passes(g, tag, bufs):
+            zb = psum.tile([P, GROUP], F32, name="zb", tag=tag, bufs=bufs)
+            for jj in range(2):
+                for c in range(2):
+                    col = jj * GROUP + c * 256
+                    nc.tensor.matmul_mx(
+                        out=zb[:, jj * 256 : (jj + 1) * 256],
+                        lhsT=wxq[:, c, :].bitcast(FP8X4),
+                        lhsT_scale=wxsc[:, c, :],
+                        rhs=xqs[g][:, col : col + 256].bitcast(FP8X4),
+                        rhs_scale=xscs[g][:, col : col + 256],
+                        start=(c == 0),
+                        stop=(c == 1),
+                    )
+            zt = work.tile([P, GROUP], F32, name="zt", tag="zt")
+            nc.scalar.activation(out=zt[:], in_=zb[:], func=ACT.Tanh, bias=pvec[:, 0:1], scale=1.0)
+            zts[g] = zt
+
+        def affine(g):
+            kT = work.tile([P, GROUP], BF16, name="kT", tag="kT")
+            nc.vector.tensor_scalar(
+                out=kT[:], in0=zts[g][:], scalar1=pvec[:, 1:2], scalar2=pvec[:, 2:3], op0=ALU.mult, op1=ALU.add
+            )
+            kTs[g] = kT
+
+        def k_transposes(g, tag, bufs):
+            kt = psum.tile([P, 4, P], BF16, name="kt", tag=tag, bufs=bufs)
+            for j in range(4):
+                nc.tensor.transpose(kt[:, j, :], kTs[g][:, j * P : (j + 1) * P], ident_b[:])
+            gk = work.tile([P, S, 4], BF16, name="gk", tag="gk", align_bytes=64)
+            eng = v_copy if g % 2 == 1 else s_copy
+            eng(out=gk[:], in_=kt[:].rearrange("p j s -> p s j"))
+            gks[g] = gk
+
+        def quant_k(g):
+            kq = const.tile([P, S], U32, name="kq%d" % g, align_bytes=64)
+            ksc = const.tile([P, S], U8, name="ksc%d" % g, align_bytes=64)
+            nc.vector.quantize_mx(
+                out=kq[:].bitcast(FP8X4), scales=ksc[:], in_=gks[g][:].rearrange("p s j -> p (s j)")
+            )
+            kqs[g], kscs[g] = kq, ksc
+
+        def kv_pass(kv, h, g, start, stop):
+            nc.tensor.matmul_mx(
+                out=kv[:],
+                lhsT=kqs[g][:].bitcast(FP8X4),
+                lhsT_scale=kscs[g][:],
+                rhs=vqs[g][:, h * 512 : (h + 1) * 512].bitcast(FP8X4),
+                rhs_scale=vscs[g][:, h * 512 : (h + 1) * 512],
+                start=start,
+                stop=stop,
+            )
+
+        def kv_out(b, h, kv, osb):
+            eng = s_copy if h == 0 else v_copy
+            eng(out=osb[:, h * 512 : (h + 1) * 512], in_=kv[:])
+            nc.sync.dma_start(out=out[b, :, h * 512 : (h + 1) * 512], in_=osb[:, h * 512 : (h + 1) * 512])
+
+        all_s = [s_copy, s_copy, s_copy, s_copy]
+        kv0, kv1 = {}, {}
+        LAST = NG - 1
+        for g in range(NG):
+            gvs[g] = work.tile([P, E, 4], BF16, name="gv", tag="gv", align_bytes=64)
+            vqs[g] = const.tile([P, E], U32, name="vq%d" % g, align_bytes=64)
+            vscs[g] = const.tile([P, E], U8, name="vsc%d" % g, align_bytes=64)
+            v_passes_adds(g, 0)
+            tanh_v(g, 0)
+            if g == 0:
+                quant_w(2)
+                nc.vector.quantize_mx(
+                    out=wxq[:].rearrange("p c n -> p (c n)").bitcast(FP8X4),
+                    scales=wxsc[:].rearrange("p c n -> p (c n)"),
+                    in_=wxg[:].rearrange("p c n t -> p (c n t)"),
+                )
+            if g >= 2:
+                quant_k(g - 2)
+            if g == LAST:
+                affine(LAST)
+                kv_out(0, 1, kv0[1], osb0)
+            v_passes_adds(g, 1)
+            if g == 0:
+                quant_w(3)
+            if g < LAST:
+                z_passes(g, "zk", 1)
+            tanh_v(g, 1)
+            if g == 0:
+                transposes(1, all_s)
+            if g == LAST:
+                k_transposes(LAST - 1, "zk", 1)
+                k_transposes(LAST, "xt", 4)
+            if 1 <= g < LAST:
+                alloc_xq(g + 1)
+                quant_x(g + 1, 0, 2 * GROUP)
+            v_passes_adds(g, 2)
+            tanh_v(g, 2)
+            if g == LAST:
+                quant_k(LAST - 1)
+                quant_k(LAST)
+            v_passes_adds(g, 3)
+            tanh_v(g, 3)
+            if g == 0:
+                alloc_xq(1)
+                quant_x(1, 0, 2 * GROUP)
+            if g < LAST:
+                if g >= 1:
+                    k_transposes(g - 1, "zk", 1)
+                if g + 2 < NG:
+                    transposes(g + 2, all_s)
+                quant_v(g, 0, 512)
+                affine(g)
+                quant_v(g, 512, 1024)
+            if g == LAST - 1:
+                z_passes(LAST, "xt", 4)
+                osb0 = work.tile([P, E], F32, name="osb", tag="osb")
+                for h in range(2):
+                    kv0[h] = psum.tile([P, 512], F32, name="kv", tag="xt", bufs=4)
+                    for gg in range(GPB):
+                        kv_pass(kv0[h], h, gg, gg == 0, gg == GPB - 1)
+                kv_out(0, 0, kv0[0], osb0)
+        osb1 = work.tile([P, E], F32, name="osb", tag="osb")
+        for h in range(2):
+            kv1[h] = psum.tile([P, 512], F32, name="kv", tag="xt", bufs=4)
+            for gg in range(GPB, LAST):
+                kv_pass(kv1[h], h, gg, gg == GPB, False)
+        quant_v(LAST, 0, 512)
+        kv_pass(kv1[0], 0, LAST, False, True)
+        kv_out(1, 0, kv1[0], osb1)
+        quant_v(LAST, 512, 768)
+        quant_v(LAST, 768, 1024)
+        kv_pass(kv1[1], 1, LAST, False, True)
+        kv_out(1, 1, kv1[1], osb1)

@@ -21,7 +21,7 @@ NQ = E // EQ
 
 FLOPS = 2 * B * NTOK * D * (E + S) + 2 * B * NTOK * S * E
 
-PIN = True
+PIN = False
 
 
 def tile_flashattention_pb_t_kernel(tc, x, Wve, bve, Wxs, bxs, gamma_k_lin, beta_k_lin, out):

@@ -22,6 +22,7 @@ NQ = E // EQ
 FLOPS = 2 * B * NTOK * D * (E + S) + 2 * B * NTOK * S * E
 
 PIN = False
+AFF_ON_G = True
 
 
 def tile_flashattention_pb_t_kernel(tc, x, Wve, bve, Wxs, bxs, gamma_k_lin, beta_k_lin, out):
@@ -218,17 +219,18 @@ def tile_flashattention_pb_t_kernel(tc, x, Wve, bve, Wxs, bxs, gamma_k_lin, beta
 
         def affine(g):
             kT = work.tile([P, GROUP], BF16, name="kT", tag="kT")
-            nc.vector.tensor_scalar(
+            eng = nc.gpsimd if AFF_ON_G else nc.vector
+            eng.tensor_scalar(
                 out=kT[:], in0=zts[g][:], scalar1=pvec[:, 1:2], scalar2=pvec[:, 2:3], op0=ALU.mult, op1=ALU.add
             )
             kTs[g] = kT
 
-        def k_transposes(g, tag, bufs):
+        def k_transposes(g, tag, bufs, on_vector):
             kt = psum.tile([P, 4, P], BF16, name="kt", tag=tag, bufs=bufs)
             for j in range(4):
                 nc.tensor.transpose(kt[:, j, :], kTs[g][:, j * P : (j + 1) * P], ident_b[:])
             gk = work.tile([P, S, 4], BF16, name="gk", tag="gk", align_bytes=64)
-            eng = v_copy if g % 2 == 1 else s_copy
+            eng = v_copy if on_vector else s_copy
             eng(out=gk[:], in_=kt[:].rearrange("p j s -> p s j"))
             gks[g] = gk
 
@@ -251,14 +253,22 @@ def tile_flashattention_pb_t_kernel(tc, x, Wve, bve, Wxs, bxs, gamma_k_lin, beta
                 stop=stop,
             )
 
-        def kv_out(b, h, kv, osb):
-            eng = s_copy if h == 0 else v_copy
+        def kv_out(b, h, kv, osb, eng):
             eng(out=osb[:, h * 512 : (h + 1) * 512], in_=kv[:])
             nc.sync.dma_start(out=out[b, :, h * 512 : (h + 1) * 512], in_=osb[:, h * 512 : (h + 1) * 512])
+
+        def quant_wx():
+            nc.vector.quantize_mx(
+                out=wxq[:].rearrange("p c n -> p (c n)").bitcast(FP8X4),
+                scales=wxsc[:].rearrange("p c n -> p (c n)"),
+                in_=wxg[:].rearrange("p c n t -> p (c n t)"),
+            )
 
         all_s = [s_copy, s_copy, s_copy, s_copy]
         kv0, kv1 = {}, {}
         LAST = NG - 1
+        osb0 = work.tile([P, E], F32, name="osb0", tag="osb")
+        osb1 = work.tile([P, E], F32, name="osb1", tag="osb")
         for g in range(NG):
             gvs[g] = work.tile([P, E, 4], BF16, name="gv", tag="gv", align_bytes=64)
             vqs[g] = const.tile([P, E], U32, name="vq%d" % g, align_bytes=64)
@@ -267,27 +277,27 @@ def tile_flashattention_pb_t_kernel(tc, x, Wve, bve, Wxs, bxs, gamma_k_lin, beta
             tanh_v(g, 0)
             if g == 0:
                 quant_w(2)
-                nc.vector.quantize_mx(
-                    out=wxq[:].rearrange("p c n -> p (c n)").bitcast(FP8X4),
-                    scales=wxsc[:].rearrange("p c n -> p (c n)"),
-                    in_=wxg[:].rearrange("p c n t -> p (c n t)"),
-                )
-            if g >= 2:
-                quant_k(g - 2)
+                quant_wx()
+            if g == 1:
+                affine(0)
             if g == LAST:
+                quant_k(LAST - 2)
                 affine(LAST)
-                kv_out(0, 1, kv0[1], osb0)
             v_passes_adds(g, 1)
             if g == 0:
                 quant_w(3)
-            if g < LAST:
+            if 1 <= g < LAST:
                 z_passes(g, "zk", 1)
             tanh_v(g, 1)
             if g == 0:
                 transposes(1, all_s)
             if g == LAST:
-                k_transposes(LAST - 1, "zk", 1)
-                k_transposes(LAST, "xt", 4)
+                k_transposes(LAST - 1, "zk", 1, False)
+                k_transposes(LAST, "xt", 4, False)
+                kv0[0] = psum.tile([P, 512], F32, name="kv", tag="xt", bufs=4)
+                for gg in range(GPB):
+                    kv_pass(kv0[0], 0, gg, gg == 0, gg == GPB - 1)
+                kv_out(0, 0, kv0[0], osb0, s_copy)
             if 1 <= g < LAST:
                 alloc_xq(g + 1)
                 quant_x(g + 1, 0, 2 * GROUP)
@@ -296,36 +306,37 @@ def tile_flashattention_pb_t_kernel(tc, x, Wve, bve, Wxs, bxs, gamma_k_lin, beta
             if g == LAST:
                 quant_k(LAST - 1)
                 quant_k(LAST)
+                kv0[1] = psum.tile([P, 512], F32, name="kv", tag="xt", bufs=4)
+                for gg in range(GPB):
+                    kv_pass(kv0[1], 1, gg, gg == 0, gg == GPB - 1)
             v_passes_adds(g, 3)
             tanh_v(g, 3)
             if g == 0:
+                z_passes(0, "zk", 1)
                 alloc_xq(1)
                 quant_x(1, 0, 2 * GROUP)
             if g < LAST:
                 if g >= 1:
-                    k_transposes(g - 1, "zk", 1)
+                    k_transposes(g - 1, "zk", 1, False)
                 if g + 2 < NG:
                     transposes(g + 2, all_s)
                 quant_v(g, 0, 512)
-                affine(g)
+                if g >= 1:
+                    affine(g)
+                if g >= 2:
+                    quant_k(g - 2)
                 quant_v(g, 512, 1024)
             if g == LAST - 1:
                 z_passes(LAST, "xt", 4)
-                osb0 = work.tile([P, E], F32, name="osb", tag="osb")
-                for h in range(2):
-                    kv0[h] = psum.tile([P, 512], F32, name="kv", tag="xt", bufs=4)
-                    for gg in range(GPB):
-                        kv_pass(kv0[h], h, gg, gg == 0, gg == GPB - 1)
-                kv_out(0, 0, kv0[0], osb0)
-        osb1 = work.tile([P, E], F32, name="osb", tag="osb")
         for h in range(2):
             kv1[h] = psum.tile([P, 512], F32, name="kv", tag="xt", bufs=4)
             for gg in range(GPB, LAST):
                 kv_pass(kv1[h], h, gg, gg == GPB, False)
         quant_v(LAST, 0, 512)
         kv_pass(kv1[0], 0, LAST, False, True)
-        kv_out(1, 0, kv1[0], osb1)
         quant_v(LAST, 512, 768)
+        kv_out(0, 1, kv0[1], osb0, s_copy)
+        kv_out(1, 0, kv1[0], osb1, s_copy)
         quant_v(LAST, 768, 1024)
         kv_pass(kv1[1], 1, LAST, False, True)
-        kv_out(1, 1, kv1[1], osb1)
+        kv_out(1, 1, kv1[1], osb1, v_copy)

@@ -18,25 +18,31 @@ NG = B * NTOK // GROUP
 GPB = NTOK // GROUP
 EQ = 256
 NQ = E // EQ
+CQ = 1
+C_TILES = 2 * CQ
+BANKS = 8
 
 FLOPS = 2 * B * NTOK * D * (E + S) + 2 * B * NTOK * S * E
-
-PIN = False
-AFF_ON_G = True
 
 
 def tile_flashattention_pb_t_kernel(tc, x, Wve, bve, Wxs, bxs, gamma_k_lin, beta_k_lin, out):
     nc = tc.nc
     with ExitStack() as ctx:
-        if PIN:
-            ctx.enter_context(tc.manual_schedule())
+        ctx.enter_context(tc.manual_schedule())
         const = ctx.enter_context(tc.tile_pool(name="const", bufs=1))
         xin = ctx.enter_context(tc.tile_pool(name="xin", bufs=4))
         work = ctx.enter_context(tc.tile_pool(name="work", bufs=2))
         psum = ctx.enter_context(tc.psum_pool(name="psum", bufs=1))
+        s_copy = nc.scalar.copy
+        v_copy = nc.vector.tensor_copy
+        X_ENG = [s_copy, v_copy, s_copy, s_copy]
 
         xv = x.rearrange("b (g p j) d -> (b g) p (j d)", g=GPB, p=P, j=4)
-        xs = {}
+        xs, gxs, xqs, xscs = {}, {}, {}, {}
+        gvs, vqs, vscs, zts, kTs, gks, kqs, kscs, us, vTs = {}, {}, {}, {}, {}, {}, {}, {}, {}, {}
+
+        def bank(shape, dtype, name):
+            return psum.tile(shape, dtype, name=name, tag="bank", bufs=BANKS)
 
         def load_x(g, pieces=1):
             t = xin.tile([P, 4 * D], BF16, name="xs", tag="xs")
@@ -47,36 +53,39 @@ def tile_flashattention_pb_t_kernel(tc, x, Wve, bve, Wxs, bxs, gamma_k_lin, beta
 
         warm = const.tile([P, 1], F32, name="warm")
         warm2 = const.tile([P, 1], F32, name="warm2")
-        rows = const.tile([P, E], BF16, name="rows")
-        small = const.tile([P, P], BF16, name="small")
+        rows = const.tile([P, E + 3 * P], BF16, name="rows")
         ones_b = const.tile([P, P], BF16, name="ones_b")
         nc.vector.memset(rows[:], 0.0)
-        nc.vector.memset(small[:], 0.0)
         nc.vector.memset(warm[:], 0.0)
         nc.vector.memset(ones_b[:], 1.0)
         nc.scalar.activation(out=warm2[:], in_=warm[:], func=ACT.Tanh)
-        load_x(0, pieces=2)
-        nc.sync.dma_start(out=rows[0:1, :], in_=bve.unsqueeze(0))
-        nc.sync.dma_start(out=small[0:1, :], in_=bxs.unsqueeze(0))
-        nc.sync.dma_start(out=small[1:2, :], in_=gamma_k_lin.unsqueeze(0))
-        nc.sync.dma_start(out=small[2:3, :], in_=beta_k_lin.unsqueeze(0))
+        wraw = [const.tile([P, 2, 4, E // 2], BF16, name="wraw%d" % h) for h in range(2)]
+        wview = Wve.rearrange("(c u p e) n -> c u p e n", c=2, u=2, p=P, e=2)
 
-        wraw = const.tile([P, 2, 4, E], BF16, name="wraw")
-        wview = Wve.rearrange("(c u p e) n -> c p u (e n)", c=2, u=2, p=P, e=2)
-        for c in range(2):
-            nc.sync.dma_start(out=wraw[:, c, :, :].rearrange("p (u e) n -> p u (e n)", u=2), in_=wview[c])
+        def load_w(h):
+            for c in range(2):
+                for u in range(2):
+                    nc.sync.dma_start(
+                        out=wraw[h][:, c, 2 * u : 2 * u + 2, :],
+                        in_=wview[c, u][:, :, h * 512 : (h + 1) * 512],
+                    )
+
+        for i, vec in enumerate((bve, bxs, gamma_k_lin, beta_k_lin)):
+            lo = 0 if i == 0 else E + (i - 1) * P
+            nc.scalar.dma_start(out=rows[0:1, lo : lo + vec.shape[0]], in_=vec.unsqueeze(0))
+        load_w(0)
+        load_x(0, pieces=2)
         wxraw = const.tile([P, 2, 4, S], BF16, name="wxraw")
         nc.sync.dma_start(
             out=wxraw[:].rearrange("p c (u e) n -> p (c u) (e n)", u=2),
             in_=Wxs.rearrange("(a p e) n -> p a (e n)", a=4, p=P, e=2),
         )
+        load_w(1)
         for g in range(1, 4):
             load_x(g)
 
         ident_f = const.tile([P, P], F32, name="ident_f")
         make_identity(nc, ident_f[:])
-        ident_b = const.tile([P, P], BF16, name="ident_b")
-        make_identity(nc, ident_b[:])
 
         wg = const.tile([P, NQ, 2, EQ, 4], BF16, name="wg", align_bytes=64)
         wq = const.tile([P, NQ, 2, EQ], U32, name="wq", align_bytes=64)
@@ -92,7 +101,7 @@ def tile_flashattention_pb_t_kernel(tc, x, Wve, bve, Wxs, bxs, gamma_k_lin, beta
             )
 
         def regroup_w(eng_copy, q, c):
-            regroup(eng_copy, wg[:, q, c, :, :], wraw[:, c, :, q * EQ : (q + 1) * EQ])
+            regroup(eng_copy, wg[:, q, c, :, :], wraw[q // 2][:, c, :, (q % 2) * EQ : (q % 2 + 1) * EQ])
 
         def quant_w(q):
             nc.vector.quantize_mx(
@@ -101,95 +110,171 @@ def tile_flashattention_pb_t_kernel(tc, x, Wve, bve, Wxs, bxs, gamma_k_lin, beta
                 in_=wg[:, q, :, :, :].rearrange("p c n t -> p (c n t)"),
             )
 
-        gxs, xqs, xscs = {}, {}, {}
+        def quant_wx():
+            nc.vector.quantize_mx(
+                out=wxq[:].rearrange("p c n -> p (c n)").bitcast(FP8X4),
+                scales=wxsc[:].rearrange("p c n -> p (c n)"),
+                in_=wxg[:].rearrange("p c n t -> p (c n t)"),
+            )
 
-        def transposes(g, copy_engines):
+        def x_transposes(g, j):
             xw = xs[g][:].bitcast(F32)
-            gx = work.tile([P, 4 * D], BF16, name="gx", tag="gx", align_bytes=64)
-            gxs[g] = gx
-            gxw = gx[:].bitcast(F32).rearrange("p (a c b t u) -> p a c b t u", a=2, c=2, b=2, t=P, u=2)
-            for j in range(4):
-                xt = psum.tile([P, 4, P], F32, name="xt", tag="xt", bufs=4)
-                for a in range(4):
-                    col = j * 512 + a * P
-                    nc.tensor.transpose(xt[:, a, :], xw[:, col : col + P], ident_f[:])
-                copy_engines[j](
-                    out=gxw[:, j // 2, :, j % 2, :, :],
-                    in_=xt[:].rearrange("p (c u) t -> p c t u", u=2),
-                )
-            if g + 4 < NG:
+            xt = bank([P, 4, P], F32, "xt")
+            for a in range(4):
+                col = j * 512 + a * P
+                nc.tensor.transpose(xt[:, a, :], xw[:, col : col + P], ident_f[:])
+            if j == 3 and g + 4 < NG:
                 load_x(g + 4)
+            return xt
 
-        def alloc_xq(g):
-            xqs[g] = work.tile([P, 2 * GROUP], U32, name="xq", tag="xq", align_bytes=64)
-            xscs[g] = work.tile([P, 2 * GROUP], U8, name="xsc", tag="xsc", align_bytes=64)
+        def x_copy(g, j, xt, eng):
+            if j == 0:
+                gxs[g] = work.tile([P, 4 * D], BF16, name="gx", tag="gx", align_bytes=64)
+                xqs[g] = work.tile([P, 2 * GROUP], U32, name="xq", tag="xq", bufs=3, align_bytes=64)
+                xscs[g] = work.tile([P, 2 * GROUP], U8, name="xsc", tag="xsc", bufs=3, align_bytes=64)
+            gxw = gxs[g][:].bitcast(F32).rearrange("p (a c b t u) -> p a c b t u", a=2, c=2, b=2, t=P, u=2)
+            eng(out=gxw[:, j // 2, :, j % 2, :, :], in_=xt[:].rearrange("p (c u) t -> p c t u", u=2))
 
-        def quant_x(g, lo, hi):
+        def quant_x(g, a):
+            lo, hi = a * GROUP, (a + 1) * GROUP
             nc.vector.quantize_mx(
                 out=xqs[g][:, lo:hi].bitcast(FP8X4), scales=xscs[g][:, lo:hi], in_=gxs[g][:, 4 * lo : 4 * hi]
             )
 
-        s_copy = nc.scalar.copy
-        v_copy = nc.vector.tensor_copy
-        transposes(0, [s_copy, v_copy, s_copy, v_copy])
-        alloc_xq(0)
-        quant_x(0, 0, GROUP)
-        quant_x(0, GROUP, 2 * GROUP)
+        def a_passes(g, q, jj):
+            vb = bank([P, 2, EQ], F32, "vb")
+            for j2 in range(2):
+                for c in range(2):
+                    col = jj * GROUP + c * 256 + j2 * P
+                    nc.tensor.matmul_mx(
+                        out=vb[:, j2, :],
+                        lhsT=xqs[g][:, col : col + P].bitcast(FP8X4),
+                        lhsT_scale=xscs[g][:, col : col + P],
+                        rhs=wq[:, q, c, :].bitcast(FP8X4),
+                        rhs_scale=wsc[:, q, c, :],
+                        start=(c == 0),
+                        stop=(c == 1),
+                    )
+            return vb
 
-        bias = const.tile([P, E], F32, name="bias")
-        for h in range(2):
-            pb = psum.tile([P, 512], F32, name="pb", tag="vb", bufs=3)
-            nc.tensor.matmul(out=pb[:], lhsT=ones_b[:], rhs=rows[:, h * 512 : (h + 1) * 512], start=True, stop=True)
-            nc.scalar.copy(out=bias[:, h * 512 : (h + 1) * 512], in_=pb[:])
-        sp = psum.tile([P, P], BF16, name="sp", tag="zk", bufs=1)
-        nc.tensor.transpose(sp[:], small[:], ident_b[:])
-        pvec = const.tile([P, 4], F32, name="pvec")
-        nc.vector.tensor_copy(out=pvec[:, 0:3], in_=sp[:, 0:3])
+        def a_add(g, q, jj, vb):
+            if jj == 0:
+                us[(g, q)] = work.tile([P, 2, EQ, 2], F32, name="u", tag="u", bufs=4)
+            nc.vector.tensor_tensor(
+                out=us[(g, q)][:, jj, :, :],
+                in0=vb[:].rearrange("p b e -> p e b"),
+                in1=bias[:, q * EQ : (q + 1) * EQ].unsqueeze(2).to_broadcast([P, EQ, 2]),
+                op=ALU.add,
+            )
 
-        regroup_w(v_copy, 0, 0)
-        regroup_w(s_copy, 2, 0)
-        regroup_w(v_copy, 1, 0)
-        regroup_w(s_copy, 3, 0)
-        regroup_w(v_copy, 0, 1)
-        regroup_w(s_copy, 2, 1)
-        quant_w(0)
-        regroup_w(v_copy, 1, 1)
-        regroup_w(s_copy, 3, 1)
-        quant_w(1)
-        for c in range(2):
-            regroup(s_copy, wxg[:, c, :, :], wxraw[:, c, :, :])
-
-        gvs, vqs, vscs, zts, kTs, gks, kqs, kscs, us = {}, {}, {}, {}, {}, {}, {}, {}, {}
-
-        def v_passes_adds(g, q):
-            u = work.tile([P, 2, EQ, 2], F32, name="u", tag="u", bufs=4)
-            us[(g, q)] = u
-            for jj in range(2):
-                vb = psum.tile([P, 2, EQ], F32, name="vb", tag="vb", bufs=3)
-                for j2 in range(2):
-                    for c in range(2):
-                        col = jj * GROUP + c * 256 + j2 * P
-                        nc.tensor.matmul_mx(
-                            out=vb[:, j2, :],
-                            lhsT=xqs[g][:, col : col + P].bitcast(FP8X4),
-                            lhsT_scale=xscs[g][:, col : col + P],
-                            rhs=wq[:, q, c, :].bitcast(FP8X4),
-                            rhs_scale=wsc[:, q, c, :],
-                            start=(c == 0),
-                            stop=(c == 1),
-                        )
-                nc.vector.tensor_tensor(
-                    out=u[:, jj, :, :],
-                    in0=vb[:].rearrange("p b e -> p e b"),
-                    in1=bias[:, q * EQ : (q + 1) * EQ].unsqueeze(2).to_broadcast([P, EQ, 2]),
-                    op=ALU.add,
-                )
-
-        def tanh_v(g, q):
+        def a_tanh(g, q):
             nc.scalar.activation(
                 out=gvs[g][:, q * EQ : (q + 1) * EQ, :].rearrange("p e (a b) -> p e a b", a=2),
                 in_=us[(g, q)][:].rearrange("p a e b -> p e a b"),
                 func=ACT.Tanh,
+            )
+
+        def e_passes(g, e0):
+            vb = bank([P, 4, P], F32, "eb")
+            q, lo = e0 // EQ, e0 % EQ
+            for j in range(4):
+                for c in range(2):
+                    col = (j // 2) * GROUP + c * 256 + (j % 2) * P
+                    nc.tensor.matmul_mx(
+                        out=vb[:, j, :],
+                        lhsT=xqs[g][:, col : col + P].bitcast(FP8X4),
+                        lhsT_scale=xscs[g][:, col : col + P],
+                        rhs=wq[:, q, c, lo : lo + P].bitcast(FP8X4),
+                        rhs_scale=wsc[:, q, c, lo : lo + P],
+                        start=(c == 0),
+                        stop=(c == 1),
+                    )
+            return vb
+
+        def e_add_tanh(g, e0, vb):
+            u = work.tile([P, P, 4], F32, name="ue", tag="ue", bufs=2)
+            nc.vector.tensor_tensor(
+                out=u[:],
+                in0=vb[:].rearrange("p j e -> p e j"),
+                in1=bias[:, e0 : e0 + P].unsqueeze(2).to_broadcast([P, P, 4]),
+                op=ALU.add,
+            )
+            nc.scalar.activation(out=gvs[g][:, e0 : e0 + P, :], in_=u[:], func=ACT.Tanh)
+
+        def t_passes(g, jj, cb, w, wscale):
+            for c in range(2):
+                col = jj * GROUP + c * 256
+                nc.tensor.matmul_mx(
+                    out=cb[:, jj * 256 : (jj + 1) * 256],
+                    lhsT=w[:, c, :].bitcast(FP8X4),
+                    lhsT_scale=wscale[:, c, :],
+                    rhs=xqs[g][:, col : col + 256].bitcast(FP8X4),
+                    rhs_scale=xscs[g][:, col : col + 256],
+                    start=(c == 0),
+                    stop=(c == 1),
+                )
+
+        def t_tanh(o, cb, i):
+            nc.scalar.activation(
+                out=o[:].rearrange("p (a t b) -> p a t b", a=2, b=2),
+                in_=cb[:].rearrange("p (a b t) -> p a t b", a=2, b=2),
+                func=ACT.Tanh,
+                bias=pvec[:, i : i + 1],
+                scale=1.0,
+            )
+
+        def c_passes(g, m, jj, cb):
+            lo = (m % 2) * P
+            t_passes(g, jj, cb, wq[:, m // 2, :, lo : lo + P], wsc[:, m // 2, :, lo : lo + P])
+
+        def c_tanh(g, m, cb):
+            vTs[(g, m)] = work.tile([P, GROUP], BF16, name="vT", tag="vT", bufs=2 * C_TILES)
+            t_tanh(vTs[(g, m)], cb, 3 + m)
+
+        def c_unit(g, m):
+            cb = bank([P, GROUP], F32, "cb")
+            for jj in range(2):
+                c_passes(g, m, jj, cb)
+            c_tanh(g, m, cb)
+
+        def z_unit(g):
+            cb = bank([P, GROUP], F32, "zb")
+            for jj in range(2):
+                t_passes(g, jj, cb, wxq, wxsc)
+            zts[g] = work.tile([P, GROUP], F32, name="zt", tag="zt")
+            t_tanh(zts[g], cb, 0)
+            kTs[g] = work.tile([P, GROUP], BF16, name="kT", tag="kT")
+            nc.gpsimd.tensor_scalar(
+                out=kTs[g][:], in0=zts[g][:], scalar1=pvec[:, 1:2], scalar2=pvec[:, 2:3], op0=ALU.mult, op1=ALU.add
+            )
+
+        def c_transposes(g):
+            ct = bank([P, C_TILES, 2, P], F32, "ct")
+            for m in range(C_TILES):
+                vw = vTs[(g, m)][:].bitcast(F32)
+                for a in range(2):
+                    nc.tensor.transpose(ct[:, m, a, :], vw[:, a * P : (a + 1) * P], ident_f[:])
+            return ct
+
+        def c_copy(g, ct, eng):
+            gvw = gvs[g][:].rearrange("p e j -> p (e j)").bitcast(F32)
+            eng(
+                out=gvw[:, 0 : 2 * C_TILES * P].rearrange("p (m e a) -> p m e a", m=C_TILES, a=2),
+                in_=ct[:].rearrange("p m a e -> p m e a"),
+            )
+
+        def k_transposes(g):
+            kt = bank([P, 2, P], F32, "kt")
+            kw = kTs[g][:].bitcast(F32)
+            for a in range(2):
+                nc.tensor.transpose(kt[:, a, :], kw[:, a * P : (a + 1) * P], ident_f[:])
+            return kt
+
+        def k_copy(g, kt, eng):
+            gks[g] = work.tile([P, S, 4], BF16, name="gk", tag="gk", align_bytes=64)
+            eng(
+                out=gks[g][:].rearrange("p s j -> p (s j)").bitcast(F32).rearrange("p (s a) -> p s a", a=2),
+                in_=kt[:].rearrange("p a s -> p s a"),
             )
 
         def quant_v(g, lo, hi):
@@ -199,144 +284,174 @@ def tile_flashattention_pb_t_kernel(tc, x, Wve, bve, Wxs, bxs, gamma_k_lin, beta
                 in_=gvs[g][:, lo:hi, :].rearrange("p e j -> p (e j)"),
             )
 
-        def z_passes(g, tag, bufs):
-            zb = psum.tile([P, GROUP], F32, name="zb", tag=tag, bufs=bufs)
-            for jj in range(2):
-                for c in range(2):
-                    col = jj * GROUP + c * 256
-                    nc.tensor.matmul_mx(
-                        out=zb[:, jj * 256 : (jj + 1) * 256],
-                        lhsT=wxq[:, c, :].bitcast(FP8X4),
-                        lhsT_scale=wxsc[:, c, :],
-                        rhs=xqs[g][:, col : col + 256].bitcast(FP8X4),
-                        rhs_scale=xscs[g][:, col : col + 256],
-                        start=(c == 0),
-                        stop=(c == 1),
-                    )
-            zt = work.tile([P, GROUP], F32, name="zt", tag="zt")
-            nc.scalar.activation(out=zt[:], in_=zb[:], func=ACT.Tanh, bias=pvec[:, 0:1], scale=1.0)
-            zts[g] = zt
-
-        def affine(g):
-            kT = work.tile([P, GROUP], BF16, name="kT", tag="kT")
-            eng = nc.gpsimd if AFF_ON_G else nc.vector
-            eng.tensor_scalar(
-                out=kT[:], in0=zts[g][:], scalar1=pvec[:, 1:2], scalar2=pvec[:, 2:3], op0=ALU.mult, op1=ALU.add
-            )
-            kTs[g] = kT
-
-        def k_transposes(g, tag, bufs, on_vector):
-            kt = psum.tile([P, 4, P], BF16, name="kt", tag=tag, bufs=bufs)
-            for j in range(4):
-                nc.tensor.transpose(kt[:, j, :], kTs[g][:, j * P : (j + 1) * P], ident_b[:])
-            gk = work.tile([P, S, 4], BF16, name="gk", tag="gk", align_bytes=64)
-            eng = v_copy if on_vector else s_copy
-            eng(out=gk[:], in_=kt[:].rearrange("p j s -> p s j"))
-            gks[g] = gk
-
         def quant_k(g):
-            kq = const.tile([P, S], U32, name="kq%d" % g, align_bytes=64)
-            ksc = const.tile([P, S], U8, name="ksc%d" % g, align_bytes=64)
+            kqs[g] = const.tile([P, S], U32, name="kq%d" % g, align_bytes=64)
+            kscs[g] = const.tile([P, S], U8, name="ksc%d" % g, align_bytes=64)
             nc.vector.quantize_mx(
-                out=kq[:].bitcast(FP8X4), scales=ksc[:], in_=gks[g][:].rearrange("p s j -> p (s j)")
+                out=kqs[g][:].bitcast(FP8X4), scales=kscs[g][:], in_=gks[g][:].rearrange("p s j -> p (s j)")
             )
-            kqs[g], kscs[g] = kq, ksc
 
-        def kv_pass(kv, h, g, start, stop):
+        def kv_pass(kv, lo, hi, g):
             nc.tensor.matmul_mx(
                 out=kv[:],
                 lhsT=kqs[g][:].bitcast(FP8X4),
                 lhsT_scale=kscs[g][:],
-                rhs=vqs[g][:, h * 512 : (h + 1) * 512].bitcast(FP8X4),
-                rhs_scale=vscs[g][:, h * 512 : (h + 1) * 512],
-                start=start,
-                stop=stop,
+                rhs=vqs[g][:, lo:hi].bitcast(FP8X4),
+                rhs_scale=vscs[g][:, lo:hi],
+                start=(g % GPB == 0),
+                stop=(g % GPB == GPB - 1),
             )
 
-        def kv_out(b, h, kv, osb, eng):
-            eng(out=osb[:, h * 512 : (h + 1) * 512], in_=kv[:])
-            nc.sync.dma_start(out=out[b, :, h * 512 : (h + 1) * 512], in_=osb[:, h * 512 : (h + 1) * 512])
+        def kv_sum(q):
+            lo, hi = q * EQ, (q + 1) * EQ
+            kv = bank([P, EQ], F32, "kv")
+            for gg in range(GPB):
+                kv_pass(kv, lo, hi, gg)
+            kv_out(0, lo, hi, kv, s_copy)
 
-        def quant_wx():
-            nc.vector.quantize_mx(
-                out=wxq[:].rearrange("p c n -> p (c n)").bitcast(FP8X4),
-                scales=wxsc[:].rearrange("p c n -> p (c n)"),
-                in_=wxg[:].rearrange("p c n t -> p (c n t)"),
-            )
+        def kv_out(b, lo, hi, kv, eng):
+            osb = work.tile([P, hi - lo], F32, name="osb", tag="osb", bufs=6)
+            eng(out=osb[:], in_=kv[:])
+            nc.sync.dma_start(out=out[b, :, lo:hi], in_=osb[:])
 
-        all_s = [s_copy, s_copy, s_copy, s_copy]
-        kv0, kv1 = {}, {}
-        LAST = NG - 1
-        osb0 = work.tile([P, E], F32, name="osb0", tag="osb")
-        osb1 = work.tile([P, E], F32, name="osb1", tag="osb")
-        for g in range(NG):
+        def a_unit(g, q, jj):
+            a_add(g, q, jj, a_passes(g, q, jj))
+
+        def new_v(g):
             gvs[g] = work.tile([P, E, 4], BF16, name="gv", tag="gv", align_bytes=64)
             vqs[g] = const.tile([P, E], U32, name="vq%d" % g, align_bytes=64)
             vscs[g] = const.tile([P, E], U8, name="vsc%d" % g, align_bytes=64)
-            v_passes_adds(g, 0)
-            tanh_v(g, 0)
-            if g == 0:
-                quant_w(2)
-                quant_wx()
-            if g == 1:
-                affine(0)
-            if g == LAST:
-                quant_k(LAST - 2)
-                affine(LAST)
-            v_passes_adds(g, 1)
-            if g == 0:
-                quant_w(3)
-            if 1 <= g < LAST:
-                z_passes(g, "zk", 1)
-            tanh_v(g, 1)
-            if g == 0:
-                transposes(1, all_s)
-            if g == LAST:
-                k_transposes(LAST - 1, "zk", 1, False)
-                k_transposes(LAST, "xt", 4, False)
-                kv0[0] = psum.tile([P, 512], F32, name="kv", tag="xt", bufs=4)
-                for gg in range(GPB):
-                    kv_pass(kv0[0], 0, gg, gg == 0, gg == GPB - 1)
-                kv_out(0, 0, kv0[0], osb0, s_copy)
-            if 1 <= g < LAST:
-                alloc_xq(g + 1)
-                quant_x(g + 1, 0, 2 * GROUP)
-            v_passes_adds(g, 2)
-            tanh_v(g, 2)
-            if g == LAST:
-                quant_k(LAST - 1)
-                quant_k(LAST)
-                kv0[1] = psum.tile([P, 512], F32, name="kv", tag="xt", bufs=4)
-                for gg in range(GPB):
-                    kv_pass(kv0[1], 1, gg, gg == 0, gg == GPB - 1)
-            v_passes_adds(g, 3)
-            tanh_v(g, 3)
-            if g == 0:
-                z_passes(0, "zk", 1)
-                alloc_xq(1)
-                quant_x(1, 0, 2 * GROUP)
-            if g < LAST:
-                if g >= 1:
-                    k_transposes(g - 1, "zk", 1, False)
-                if g + 2 < NG:
-                    transposes(g + 2, all_s)
-                quant_v(g, 0, 512)
-                if g >= 1:
-                    affine(g)
-                if g >= 2:
-                    quant_k(g - 2)
-                quant_v(g, 512, 1024)
-            if g == LAST - 1:
-                z_passes(LAST, "xt", 4)
+
+        regroup_w(v_copy, 0, 0)
+        regroup_w(s_copy, 1, 0)
+        regroup_w(v_copy, 0, 1)
+        regroup_w(s_copy, 1, 1)
+        quant_w(0)
+        new_v(0)
+        xts = [x_transposes(0, j) for j in range(2)]
+        sp = bank([P, 3 + C_TILES], F32, "sp")
+        for i in range(3 + C_TILES):
+            lo = E + i * P if i < 3 else (i - 3) * P
+            nc.tensor.matmul(
+                out=sp[:, i : i + 1], lhsT=rows[:, lo : lo + P], rhs=ones_b[:, 0:1], start=True, stop=True
+            )
+        bias = const.tile([P, E], F32, name="bias")
+        pbs = []
         for h in range(2):
-            kv1[h] = psum.tile([P, 512], F32, name="kv", tag="xt", bufs=4)
-            for gg in range(GPB, LAST):
-                kv_pass(kv1[h], h, gg, gg == GPB, False)
-        quant_v(LAST, 0, 512)
-        kv_pass(kv1[0], 0, LAST, False, True)
-        quant_v(LAST, 512, 768)
-        kv_out(0, 1, kv0[1], osb0, s_copy)
-        kv_out(1, 0, kv1[0], osb1, s_copy)
-        quant_v(LAST, 768, 1024)
-        kv_pass(kv1[1], 1, LAST, False, True)
-        kv_out(1, 1, kv1[1], osb1, v_copy)
+            pbs.append(bank([P, 512], F32, "pb"))
+            nc.tensor.matmul(out=pbs[h][:], lhsT=ones_b[:], rhs=rows[:, h * 512 : (h + 1) * 512], start=True, stop=True)
+        x_copy(0, 0, xts[0], v_copy)
+        x_copy(0, 1, xts[1], s_copy)
+        quant_w(1)
+        quant_x(0, 0)
+        xts = [x_transposes(0, j) for j in range(2, 4)]
+        nc.scalar.copy(out=bias[:, 0:512], in_=pbs[0][:])
+        x_copy(0, 2, xts[0], s_copy)
+        x_copy(0, 3, xts[1], v_copy)
+        for c in range(2):
+            regroup(v_copy, wxg[:, c, :, :], wxraw[:, c, :, :])
+        quant_x(0, 1)
+        vb = a_passes(0, 1, 0)
+        cbs = [bank([P, GROUP], F32, "cb") for m in range(C_TILES)]
+        for jj in range(2):
+            for m in range(C_TILES):
+                c_passes(0, m, jj, cbs[m])
+        pvec = const.tile([P, 3 + C_TILES], F32, name="pvec")
+        nc.vector.tensor_copy(out=pvec[:], in_=sp[:])
+        a_add(0, 1, 0, vb)
+        quant_wx()
+        nc.scalar.copy(out=bias[:, 512:1024], in_=pbs[1][:])
+        regroup_w(v_copy, 2, 0)
+        regroup_w(s_copy, 3, 0)
+        regroup_w(v_copy, 2, 1)
+        regroup_w(s_copy, 3, 1)
+        a_unit(0, 1, 1)
+        for m in range(C_TILES):
+            c_tanh(0, m, cbs[m])
+        z_unit(0)
+        quant_w(2)
+        a_tanh(0, 1)
+        xts = [x_transposes(1, j) for j in range(4)]
+        quant_w(3)
+        x_copy(1, 0, xts[0], s_copy)
+        x_copy(1, 1, xts[1], v_copy)
+        a_unit(0, 2, 0)
+        x_copy(1, 2, xts[2], s_copy)
+        a_unit(0, 2, 1)
+        x_copy(1, 3, xts[3], s_copy)
+        quant_x(1, 0)
+        a_tanh(0, 2)
+        a_unit(0, 3, 0)
+        quant_x(1, 1)
+        a_unit(0, 3, 1)
+
+        for g in range(1, NG - 1):
+            xts = [x_transposes(g + 1, j) for j in range(4)]
+            kt = k_transposes(g - 1)
+            ct = c_transposes(g - 1)
+            for j in range(3):
+                x_copy(g + 1, j, xts[j], X_ENG[j])
+            a_tanh(g - 1, 3)
+            x_copy(g + 1, 3, xts[3], X_ENG[3])
+            c_copy(g - 1, ct, v_copy)
+            k_copy(g - 1, kt, s_copy)
+            new_v(g)
+            a_unit(g, 1, 0)
+            quant_x(g + 1, 0)
+            z_unit(g)
+            a_unit(g, 1, 1)
+            quant_v(g - 1, 0, 512)
+            c_unit(g, 0)
+            a_tanh(g, 1)
+            a_unit(g, 2, 0)
+            quant_k(g - 1)
+            quant_x(g + 1, 1)
+            c_unit(g, 1)
+            a_unit(g, 2, 1)
+            quant_v(g - 1, 512, 1024)
+            a_tanh(g, 2)
+            if g >= GPB:
+                kv_sum(g - GPB)
+            a_unit(g, 3, 0)
+            a_unit(g, 3, 1)
+
+        g = NG - 1
+        kt = k_transposes(g - 1)
+        ct = c_transposes(g - 1)
+        a_tanh(g - 1, 3)
+        k_copy(g - 1, kt, s_copy)
+        c_copy(g - 1, ct, v_copy)
+        new_v(g)
+        z_unit(g)
+        for m in range(C_TILES):
+            c_unit(g, m)
+        quant_v(g - 1, 0, 512)
+        quant_k(g - 1)
+        a_unit(g, 1, 0)
+        a_unit(g, 1, 1)
+        a_tanh(g, 1)
+        quant_v(g - 1, 512, 1024)
+        kv_sum(g - GPB)
+        a_unit(g, 2, 0)
+        kt = k_transposes(g)
+        ct = c_transposes(g)
+        k_copy(g, kt, s_copy)
+        c_copy(g, ct, s_copy)
+        a_unit(g, 2, 1)
+        a_tanh(g, 2)
+        for e0 in (3 * EQ, 3 * EQ + P):
+            e_add_tanh(g, e0, e_passes(g, e0))
+        quant_k(g)
+        quant_v(g, 0, 512)
+        cuts = [(0, 512), (512, 768), (768, 896), (896, 1024)]
+        kvb = {}
+        for lo, hi in cuts:
+            kvb[lo] = bank([P, hi - lo], F32, "kv")
+            for gg in range(GPB, g):
+                kv_pass(kvb[lo], lo, hi, gg)
+        for lo, hi in cuts:
+            if lo:
+                quant_v(g, lo, hi)
+            kv_pass(kvb[lo], lo, hi, g)
+        for lo, hi in cuts:
+            kv_out(1, lo, hi, kvb[lo], v_copy if lo == 768 else s_copy)

@@ -18,9 +18,9 @@ NG = B * NTOK // GROUP
 GPB = NTOK // GROUP
 EQ = 256
 NQ = E // EQ
-CQ = 1
-C_TILES = 2 * CQ
+C_TILES = 4
 BANKS = 8
+DVE0 = 4
 
 FLOPS = 2 * B * NTOK * D * (E + S) + 2 * B * NTOK * S * E
 
@@ -45,11 +45,22 @@ def tile_flashattention_pb_t_kernel(tc, x, Wve, bve, Wxs, bxs, gamma_k_lin, beta
             return psum.tile(shape, dtype, name=name, tag="bank", bufs=BANKS)
 
         def load_x(g, pieces=1):
-            t = xin.tile([P, 4 * D], BF16, name="xs", tag="xs")
-            w = 4 * D // pieces
-            for i in range(pieces):
-                nc.sync.dma_start(out=t[:, i * w : (i + 1) * w], in_=xv[g][:, i * w : (i + 1) * w])
+            t = xin.tile([P, 4 * D], BF16, name="xs", tag="xs", align_bytes=64)
             xs[g] = t
+            if g < DVE0:
+                w = 4 * D // pieces
+                for i in range(pieces):
+                    nc.sync.dma_start(out=t[:, i * w : (i + 1) * w], in_=xv[g][:, i * w : (i + 1) * w])
+                return
+            xb = x[g // GPB, (g % GPB) * GROUP : (g % GPB + 1) * GROUP, :]
+            for c in range(2):
+                for h in range(2):
+                    for a in range(4):
+                        d0 = 512 * c + 256 * h + 64 * a
+                        nc.sync.dma_start(
+                            out=t[32 * a + h : 32 * a + 32 : 2, c * 2 * D : (c + 1) * 2 * D].rearrange("p (k d) -> p k d", d=64),
+                            in_=xb[:, d0 : d0 + 64].rearrange("(k t) d -> t k d", t=16),
+                        )
 
         warm = const.tile([P, 1], F32, name="warm")
         warm2 = const.tile([P, 1], F32, name="warm2")
@@ -123,15 +134,25 @@ def tile_flashattention_pb_t_kernel(tc, x, Wve, bve, Wxs, bxs, gamma_k_lin, beta
             for a in range(4):
                 col = j * 512 + a * P
                 nc.tensor.transpose(xt[:, a, :], xw[:, col : col + P], ident_f[:])
-            if j == 3 and g + 4 < NG:
-                load_x(g + 4)
             return xt
+
+        def new_x(g):
+            gxs[g] = work.tile([P, 4 * D], BF16, name="gx", tag="gx", align_bytes=64)
+            xqs[g] = work.tile([P, 2 * GROUP], U32, name="xq", tag="xq", bufs=3, align_bytes=64)
+            xscs[g] = work.tile([P, 2 * GROUP], U8, name="xsc", tag="xsc", bufs=3, align_bytes=64)
+
+        def x_blocks(g, c):
+            lo, hi = c * D, (c + 1) * D
+            nc.vector.transpose(out=gxs[g][:].bitcast(F32)[:, lo:hi], in_=xs[g][:].bitcast(F32)[:, lo:hi])
+
+        def xcol(g, c, j):
+            if g >= DVE0:
+                return c * GROUP + j * P
+            return (j // 2) * GROUP + c * 256 + (j % 2) * P
 
         def x_copy(g, j, xt, eng):
             if j == 0:
-                gxs[g] = work.tile([P, 4 * D], BF16, name="gx", tag="gx", align_bytes=64)
-                xqs[g] = work.tile([P, 2 * GROUP], U32, name="xq", tag="xq", bufs=3, align_bytes=64)
-                xscs[g] = work.tile([P, 2 * GROUP], U8, name="xsc", tag="xsc", bufs=3, align_bytes=64)
+                new_x(g)
             gxw = gxs[g][:].bitcast(F32).rearrange("p (a c b t u) -> p a c b t u", a=2, c=2, b=2, t=P, u=2)
             eng(out=gxw[:, j // 2, :, j % 2, :, :], in_=xt[:].rearrange("p (c u) t -> p c t u", u=2))
 
@@ -145,7 +166,7 @@ def tile_flashattention_pb_t_kernel(tc, x, Wve, bve, Wxs, bxs, gamma_k_lin, beta
             vb = bank([P, 2, EQ], F32, "vb")
             for j2 in range(2):
                 for c in range(2):
-                    col = jj * GROUP + c * 256 + j2 * P
+                    col = xcol(g, c, 2 * jj + j2)
                     nc.tensor.matmul_mx(
                         out=vb[:, j2, :],
                         lhsT=xqs[g][:, col : col + P].bitcast(FP8X4),
@@ -179,7 +200,7 @@ def tile_flashattention_pb_t_kernel(tc, x, Wve, bve, Wxs, bxs, gamma_k_lin, beta
             q, lo = e0 // EQ, e0 % EQ
             for j in range(4):
                 for c in range(2):
-                    col = (j // 2) * GROUP + c * 256 + (j % 2) * P
+                    col = xcol(g, c, j)
                     nc.tensor.matmul_mx(
                         out=vb[:, j, :],
                         lhsT=xqs[g][:, col : col + P].bitcast(FP8X4),
@@ -203,7 +224,7 @@ def tile_flashattention_pb_t_kernel(tc, x, Wve, bve, Wxs, bxs, gamma_k_lin, beta
 
         def t_passes(g, jj, cb, w, wscale):
             for c in range(2):
-                col = jj * GROUP + c * 256
+                col = xcol(g, c, 2 * jj)
                 nc.tensor.matmul_mx(
                     out=cb[:, jj * 256 : (jj + 1) * 256],
                     lhsT=w[:, c, :].bitcast(FP8X4),
@@ -228,7 +249,7 @@ def tile_flashattention_pb_t_kernel(tc, x, Wve, bve, Wxs, bxs, gamma_k_lin, beta
             t_passes(g, jj, cb, wq[:, m // 2, :, lo : lo + P], wsc[:, m // 2, :, lo : lo + P])
 
         def c_tanh(g, m, cb):
-            vTs[(g, m)] = work.tile([P, GROUP], BF16, name="vT", tag="vT", bufs=2 * C_TILES)
+            vTs[(g, m)] = work.tile([P, GROUP], BF16, name="vT", tag="vT", bufs=6)
             t_tanh(vTs[(g, m)], cb, 3 + m)
 
         def c_unit(g, m):
@@ -248,18 +269,24 @@ def tile_flashattention_pb_t_kernel(tc, x, Wve, bve, Wxs, bxs, gamma_k_lin, beta
                 out=kTs[g][:], in0=zts[g][:], scalar1=pvec[:, 1:2], scalar2=pvec[:, 2:3], op0=ALU.mult, op1=ALU.add
             )
 
-        def c_transposes(g):
-            ct = bank([P, C_TILES, 2, P], F32, "ct")
-            for m in range(C_TILES):
-                vw = vTs[(g, m)][:].bitcast(F32)
-                for a in range(2):
-                    nc.tensor.transpose(ct[:, m, a, :], vw[:, a * P : (a + 1) * P], ident_f[:])
-            return ct
+        def c_quarters(g):
+            return 2 if DVE0 <= g + 1 < NG else 1
 
-        def c_copy(g, ct, eng):
+        def c_transposes(g):
+            cts = []
+            for q in range(c_quarters(g)):
+                ct = bank([P, 2, 2, P], F32, "ct")
+                for m in range(2):
+                    vw = vTs[(g, 2 * q + m)][:].bitcast(F32)
+                    for a in range(2):
+                        nc.tensor.transpose(ct[:, m, a, :], vw[:, a * P : (a + 1) * P], ident_f[:])
+                cts.append(ct)
+            return cts
+
+        def c_copy(g, q, ct, eng):
             gvw = gvs[g][:].rearrange("p e j -> p (e j)").bitcast(F32)
             eng(
-                out=gvw[:, 0 : 2 * C_TILES * P].rearrange("p (m e a) -> p m e a", m=C_TILES, a=2),
+                out=gvw[:, 2 * q * EQ : 2 * (q + 1) * EQ].rearrange("p (m e a) -> p m e a", m=2, a=2),
                 in_=ct[:].rearrange("p m a e -> p m e a"),
             )
 
@@ -352,9 +379,9 @@ def tile_flashattention_pb_t_kernel(tc, x, Wve, bve, Wxs, bxs, gamma_k_lin, beta
             regroup(v_copy, wxg[:, c, :, :], wxraw[:, c, :, :])
         quant_x(0, 1)
         vb = a_passes(0, 1, 0)
-        cbs = [bank([P, GROUP], F32, "cb") for m in range(C_TILES)]
+        cbs = [bank([P, GROUP], F32, "cb") for m in range(2)]
         for jj in range(2):
-            for m in range(C_TILES):
+            for m in range(2):
                 c_passes(0, m, jj, cbs[m])
         pvec = const.tile([P, 3 + C_TILES], F32, name="pvec")
         nc.vector.tensor_copy(out=pvec[:], in_=sp[:])
@@ -366,7 +393,7 @@ def tile_flashattention_pb_t_kernel(tc, x, Wve, bve, Wxs, bxs, gamma_k_lin, beta
         regroup_w(v_copy, 2, 1)
         regroup_w(s_copy, 3, 1)
         a_unit(0, 1, 1)
-        for m in range(C_TILES):
+        for m in range(2):
             c_tanh(0, m, cbs[m])
         z_unit(0)
         quant_w(2)
@@ -385,15 +412,16 @@ def tile_flashattention_pb_t_kernel(tc, x, Wve, bve, Wxs, bxs, gamma_k_lin, beta
         quant_x(1, 1)
         a_unit(0, 3, 1)
 
-        for g in range(1, NG - 1):
+        load_x(4)
+        for g in range(1, DVE0 - 1):
             xts = [x_transposes(g + 1, j) for j in range(4)]
             kt = k_transposes(g - 1)
-            ct = c_transposes(g - 1)
+            cts = c_transposes(g - 1)
             for j in range(3):
                 x_copy(g + 1, j, xts[j], X_ENG[j])
             a_tanh(g - 1, 3)
             x_copy(g + 1, 3, xts[3], X_ENG[3])
-            c_copy(g - 1, ct, v_copy)
+            c_copy(g - 1, 0, cts[0], v_copy)
             k_copy(g - 1, kt, s_copy)
             new_v(g)
             a_unit(g, 1, 0)
@@ -410,20 +438,57 @@ def tile_flashattention_pb_t_kernel(tc, x, Wve, bve, Wxs, bxs, gamma_k_lin, beta
             a_unit(g, 2, 1)
             quant_v(g - 1, 512, 1024)
             a_tanh(g, 2)
-            if g >= GPB:
-                kv_sum(g - GPB)
+            if g > GPB:
+                kv_sum(g - GPB - 1)
             a_unit(g, 3, 0)
             a_unit(g, 3, 1)
+            if g + 4 < NG:
+                load_x(g + 4)
+        for g in range(DVE0 - 1, NG - 1):
+            if g == DVE0 - 1:
+                new_x(g + 1)
+                x_blocks(g + 1, 0)
+            a_tanh(g - 1, 3)
+            new_v(g)
+            a_unit(g, 2, 0)
+            z_unit(g)
+            kt = k_transposes(g - 1)
+            cts = c_transposes(g - 1)
+            for q, ct in enumerate(cts):
+                c_copy(g - 1, q, ct, s_copy)
+            k_copy(g - 1, kt, s_copy)
+            x_blocks(g + 1, 1)
+            c_unit(g, 0)
+            a_unit(g, 2, 1)
+            a_tanh(g, 2)
+            quant_x(g + 1, 0)
+            quant_v(g - 1, 512, 1024)
+            c_unit(g, 1)
+            a_unit(g, 3, 0)
+            quant_x(g + 1, 1)
+            quant_v(g - 1, 0, 512)
+            c_unit(g, 2)
+            quant_k(g - 1)
+            if g > GPB:
+                kv_sum(g - GPB - 1)
+            c_unit(g, 3)
+            a_unit(g, 3, 1)
+            if g + 2 < NG:
+                new_x(g + 2)
+                x_blocks(g + 2, 0)
+            if g + 4 < NG:
+                load_x(g + 4)
 
         g = NG - 1
-        kt = k_transposes(g - 1)
-        ct = c_transposes(g - 1)
         a_tanh(g - 1, 3)
-        k_copy(g - 1, kt, s_copy)
-        c_copy(g - 1, ct, v_copy)
         new_v(g)
         z_unit(g)
-        for m in range(C_TILES):
+        kt = k_transposes(g - 1)
+        cts = c_transposes(g - 1)
+        k_copy(g - 1, kt, s_copy)
+        for q, ct in enumerate(cts):
+            c_copy(g - 1, q, ct, v_copy)
+        for m in range(2):
             c_unit(g, m)
         quant_v(g - 1, 0, 512)
         quant_k(g - 1)
@@ -431,12 +496,13 @@ def tile_flashattention_pb_t_kernel(tc, x, Wve, bve, Wxs, bxs, gamma_k_lin, beta
         a_unit(g, 1, 1)
         a_tanh(g, 1)
         quant_v(g - 1, 512, 1024)
-        kv_sum(g - GPB)
+        for q in (2, 3):
+            kv_sum(q)
         a_unit(g, 2, 0)
         kt = k_transposes(g)
-        ct = c_transposes(g)
+        cts = c_transposes(g)
         k_copy(g, kt, s_copy)
-        c_copy(g, ct, s_copy)
+        c_copy(g, 0, cts[0], s_copy)
         a_unit(g, 2, 1)
         a_tanh(g, 2)
         for e0 in (3 * EQ, 3 * EQ + P):

@@ -18,9 +18,9 @@ NG = B * NTOK // GROUP
 GPB = NTOK // GROUP
 EQ = 256
 NQ = E // EQ
-C_TILES = 4
+C_TILES = 6
 BANKS = 8
-DVE0 = 4
+DVE0 = 3
 
 FLOPS = 2 * B * NTOK * D * (E + S) + 2 * B * NTOK * S * E
 
@@ -249,7 +249,7 @@ def tile_flashattention_pb_t_kernel(tc, x, Wve, bve, Wxs, bxs, gamma_k_lin, beta
             t_passes(g, jj, cb, wq[:, m // 2, :, lo : lo + P], wsc[:, m // 2, :, lo : lo + P])
 
         def c_tanh(g, m, cb):
-            vTs[(g, m)] = work.tile([P, GROUP], BF16, name="vT", tag="vT", bufs=6)
+            vTs[(g, m)] = work.tile([P, GROUP], BF16, name="vT", tag="vT", bufs=8)
             t_tanh(vTs[(g, m)], cb, 3 + m)
 
         def c_unit(g, m):
@@ -270,7 +270,7 @@ def tile_flashattention_pb_t_kernel(tc, x, Wve, bve, Wxs, bxs, gamma_k_lin, beta
             )
 
         def c_quarters(g):
-            return 2 if DVE0 <= g + 1 < NG else 1
+            return 3 if DVE0 <= g + 1 < NG else 1
 
         def c_transposes(g):
             cts = []
@@ -372,7 +372,7 @@ def tile_flashattention_pb_t_kernel(tc, x, Wve, bve, Wxs, bxs, gamma_k_lin, beta
         quant_w(1)
         quant_x(0, 0)
         xts = [x_transposes(0, j) for j in range(2, 4)]
-        nc.scalar.copy(out=bias[:, 0:512], in_=pbs[0][:])
+        nc.scalar.copy(out=bias[:, EQ:512], in_=pbs[0][:, EQ:512])
         x_copy(0, 2, xts[0], s_copy)
         x_copy(0, 3, xts[1], v_copy)
         for c in range(2):
@@ -449,33 +449,32 @@ def tile_flashattention_pb_t_kernel(tc, x, Wve, bve, Wxs, bxs, gamma_k_lin, beta
                 new_x(g + 1)
                 x_blocks(g + 1, 0)
             a_tanh(g - 1, 3)
+            x_blocks(g + 1, 1)
             new_v(g)
-            a_unit(g, 2, 0)
             z_unit(g)
+            c_unit(g, 0)
+            a_unit(g, 3, 0)
             kt = k_transposes(g - 1)
             cts = c_transposes(g - 1)
-            for q, ct in enumerate(cts):
-                c_copy(g - 1, q, ct, s_copy)
             k_copy(g - 1, kt, s_copy)
-            x_blocks(g + 1, 1)
-            c_unit(g, 0)
-            a_unit(g, 2, 1)
-            a_tanh(g, 2)
+            for q, ct in enumerate(cts):
+                c_copy(g - 1, q, ct, v_copy if q == 0 else s_copy)
             quant_x(g + 1, 0)
-            quant_v(g - 1, 512, 1024)
             c_unit(g, 1)
-            a_unit(g, 3, 0)
-            quant_x(g + 1, 1)
-            quant_v(g - 1, 0, 512)
             c_unit(g, 2)
+            a_unit(g, 3, 1)
+            quant_x(g + 1, 1)
+            quant_v(g - 1, 512, 1024)
+            c_unit(g, 3)
+            quant_v(g - 1, 0, 512)
             quant_k(g - 1)
             if g > GPB:
                 kv_sum(g - GPB - 1)
-            c_unit(g, 3)
-            a_unit(g, 3, 1)
+            c_unit(g, 4)
             if g + 2 < NG:
                 new_x(g + 2)
                 x_blocks(g + 2, 0)
+            c_unit(g, 5)
             if g + 4 < NG:
                 load_x(g + 4)
 
@@ -487,7 +486,7 @@ def tile_flashattention_pb_t_kernel(tc, x, Wve, bve, Wxs, bxs, gamma_k_lin, beta
         cts = c_transposes(g - 1)
         k_copy(g - 1, kt, s_copy)
         for q, ct in enumerate(cts):
-            c_copy(g - 1, q, ct, v_copy)
+            c_copy(g - 1, q, ct, s_copy if q == 2 else v_copy)
         for m in range(2):
             c_unit(g, m)
         quant_v(g - 1, 0, 512)

@@ -20,7 +20,7 @@ EQ = 256
 NQ = E // EQ
 C_TILES = 6
 BANKS = 8
-DVE0 = 3
+DVE0 = 4
 
 FLOPS = 2 * B * NTOK * D * (E + S) + 2 * B * NTOK * S * E
 

@@ -21,6 +21,7 @@ NQ = E // EQ
 C_TILES = 6
 BANKS = 8
 DVE0 = 4
+CQS = [1, 1, 1, 3, 3, 3, 2, 0]
 
 FLOPS = 2 * B * NTOK * D * (E + S) + 2 * B * NTOK * S * E
 
@@ -35,7 +36,7 @@ def tile_flashattention_pb_t_kernel(tc, x, Wve, bve, Wxs, bxs, gamma_k_lin, beta
         psum = ctx.enter_context(tc.psum_pool(name="psum", bufs=1))
         s_copy = nc.scalar.copy
         v_copy = nc.vector.tensor_copy
-        X_ENG = [s_copy, v_copy, s_copy, s_copy]
+        X_ENG = [s_copy, s_copy, s_copy, s_copy]
 
         xv = x.rearrange("b (g p j) d -> (b g) p (j d)", g=GPB, p=P, j=4)
         xs, gxs, xqs, xscs = {}, {}, {}, {}
@@ -44,13 +45,12 @@ def tile_flashattention_pb_t_kernel(tc, x, Wve, bve, Wxs, bxs, gamma_k_lin, beta
         def bank(shape, dtype, name):
             return psum.tile(shape, dtype, name=name, tag="bank", bufs=BANKS)
 
-        def load_x(g, pieces=1):
+        def load_x(g, pieces=((0, 4),)):
             t = xin.tile([P, 4 * D], BF16, name="xs", tag="xs", align_bytes=64)
             xs[g] = t
             if g < DVE0:
-                w = 4 * D // pieces
-                for i in range(pieces):
-                    nc.sync.dma_start(out=t[:, i * w : (i + 1) * w], in_=xv[g][:, i * w : (i + 1) * w])
+                for lo, hi in pieces:
+                    nc.sync.dma_start(out=t[:, lo * D : hi * D], in_=xv[g][:, lo * D : hi * D])
                 return
             xb = x[g // GPB, (g % GPB) * GROUP : (g % GPB + 1) * GROUP, :]
             for c in range(2):
@@ -85,14 +85,15 @@ def tile_flashattention_pb_t_kernel(tc, x, Wve, bve, Wxs, bxs, gamma_k_lin, beta
             lo = 0 if i == 0 else E + (i - 1) * P
             nc.scalar.dma_start(out=rows[0:1, lo : lo + vec.shape[0]], in_=vec.unsqueeze(0))
         load_w(0)
-        load_x(0, pieces=2)
+        load_x(0, ((0, 1), (1, 2), (2, 4)))
         wxraw = const.tile([P, 2, 4, S], BF16, name="wxraw")
         nc.sync.dma_start(
             out=wxraw[:].rearrange("p c (u e) n -> p (c u) (e n)", u=2),
             in_=Wxs.rearrange("(a p e) n -> p a (e n)", a=4, p=P, e=2),
         )
         load_w(1)
-        for g in range(1, 4):
+        load_x(1, ((0, 2), (2, 4)))
+        for g in range(2, 4):
             load_x(g)
 
         ident_f = const.tile([P, P], F32, name="ident_f")
@@ -141,8 +142,10 @@ def tile_flashattention_pb_t_kernel(tc, x, Wve, bve, Wxs, bxs, gamma_k_lin, beta
             xqs[g] = work.tile([P, 2 * GROUP], U32, name="xq", tag="xq", bufs=3, align_bytes=64)
             xscs[g] = work.tile([P, 2 * GROUP], U8, name="xsc", tag="xsc", bufs=3, align_bytes=64)
 
-        def x_blocks(g, c):
-            lo, hi = c * D, (c + 1) * D
+        def x_blocks(g, half=None):
+            if not half:
+                new_x(g)
+            lo, hi = (0, 2 * D) if half is None else (half * D, (half + 1) * D)
             nc.vector.transpose(out=gxs[g][:].bitcast(F32)[:, lo:hi], in_=xs[g][:].bitcast(F32)[:, lo:hi])
 
         def xcol(g, c, j):
@@ -156,8 +159,8 @@ def tile_flashattention_pb_t_kernel(tc, x, Wve, bve, Wxs, bxs, gamma_k_lin, beta
             gxw = gxs[g][:].bitcast(F32).rearrange("p (a c b t u) -> p a c b t u", a=2, c=2, b=2, t=P, u=2)
             eng(out=gxw[:, j // 2, :, j % 2, :, :], in_=xt[:].rearrange("p (c u) t -> p c t u", u=2))
 
-        def quant_x(g, a):
-            lo, hi = a * GROUP, (a + 1) * GROUP
+        def quant_x(g, a=None):
+            lo, hi = (0, 2 * GROUP) if a is None else (a * GROUP, (a + 1) * GROUP)
             nc.vector.quantize_mx(
                 out=xqs[g][:, lo:hi].bitcast(FP8X4), scales=xscs[g][:, lo:hi], in_=gxs[g][:, 4 * lo : 4 * hi]
             )
@@ -270,7 +273,7 @@ def tile_flashattention_pb_t_kernel(tc, x, Wve, bve, Wxs, bxs, gamma_k_lin, beta
             )
 
         def c_quarters(g):
-            return 3 if DVE0 <= g + 1 < NG else 1
+            return CQS[g]
 
         def c_transposes(g):
             cts = []
@@ -329,12 +332,14 @@ def tile_flashattention_pb_t_kernel(tc, x, Wve, bve, Wxs, bxs, gamma_k_lin, beta
                 stop=(g % GPB == GPB - 1),
             )
 
-        def kv_sum(q):
-            lo, hi = q * EQ, (q + 1) * EQ
+        def kv_passes(q):
             kv = bank([P, EQ], F32, "kv")
             for gg in range(GPB):
-                kv_pass(kv, lo, hi, gg)
-            kv_out(0, lo, hi, kv, s_copy)
+                kv_pass(kv, q * EQ, (q + 1) * EQ, gg)
+            return kv
+
+        def kv_sum(q):
+            kv_out(0, q * EQ, (q + 1) * EQ, kv_passes(q), s_copy)
 
         def kv_out(b, lo, hi, kv, eng):
             osb = work.tile([P, hi - lo], F32, name="osb", tag="osb", bufs=6)
@@ -372,7 +377,7 @@ def tile_flashattention_pb_t_kernel(tc, x, Wve, bve, Wxs, bxs, gamma_k_lin, beta
         quant_w(1)
         quant_x(0, 0)
         xts = [x_transposes(0, j) for j in range(2, 4)]
-        nc.scalar.copy(out=bias[:, EQ:512], in_=pbs[0][:, EQ:512])
+        nc.scalar.copy(out=bias[:, 0:512], in_=pbs[0][:])
         x_copy(0, 2, xts[0], s_copy)
         x_copy(0, 3, xts[1], v_copy)
         for c in range(2):
@@ -417,6 +422,8 @@ def tile_flashattention_pb_t_kernel(tc, x, Wve, bve, Wxs, bxs, gamma_k_lin, beta
             xts = [x_transposes(g + 1, j) for j in range(4)]
             kt = k_transposes(g - 1)
             cts = c_transposes(g - 1)
+            if g + 2 == DVE0:
+                x_blocks(g + 2, 0)
             for j in range(3):
                 x_copy(g + 1, j, xts[j], X_ENG[j])
             a_tanh(g - 1, 3)
@@ -438,76 +445,80 @@ def tile_flashattention_pb_t_kernel(tc, x, Wve, bve, Wxs, bxs, gamma_k_lin, beta
             a_unit(g, 2, 1)
             quant_v(g - 1, 512, 1024)
             a_tanh(g, 2)
-            if g > GPB:
-                kv_sum(g - GPB - 1)
             a_unit(g, 3, 0)
             a_unit(g, 3, 1)
             if g + 4 < NG:
                 load_x(g + 4)
         for g in range(DVE0 - 1, NG - 1):
-            if g == DVE0 - 1:
-                new_x(g + 1)
-                x_blocks(g + 1, 0)
+            cq = c_quarters(g)
             a_tanh(g - 1, 3)
             x_blocks(g + 1, 1)
             new_v(g)
             z_unit(g)
             c_unit(g, 0)
-            a_unit(g, 3, 0)
+            a_unit(g, cq, 0)
             kt = k_transposes(g - 1)
             cts = c_transposes(g - 1)
             k_copy(g - 1, kt, s_copy)
             for q, ct in enumerate(cts):
-                c_copy(g - 1, q, ct, v_copy if q == 0 else s_copy)
+                c_copy(g - 1, q, ct, v_copy if q == 0 and cq == 3 else s_copy)
             quant_x(g + 1, 0)
             c_unit(g, 1)
-            c_unit(g, 2)
-            a_unit(g, 3, 1)
+            if cq == 3:
+                c_unit(g, 2)
+                a_unit(g, 3, 1)
+            else:
+                a_unit(g, 2, 1)
+                a_tanh(g, 2)
+                c_unit(g, 2)
             quant_x(g + 1, 1)
             quant_v(g - 1, 512, 1024)
-            c_unit(g, 3)
+            if cq == 3:
+                c_unit(g, 3)
+            else:
+                a_unit(g, 3, 0)
             quant_v(g - 1, 0, 512)
             quant_k(g - 1)
             if g > GPB:
                 kv_sum(g - GPB - 1)
-            c_unit(g, 4)
-            if g + 2 < NG:
-                new_x(g + 2)
-                x_blocks(g + 2, 0)
-            c_unit(g, 5)
+            c_unit(g, 4 if cq == 3 else 3)
+            if cq == 3:
+                if g + 2 < NG:
+                    x_blocks(g + 2, 0)
+                c_unit(g, 5)
+            else:
+                a_unit(g, 3, 1)
+                if g + 2 < NG:
+                    x_blocks(g + 2, 0)
             if g + 4 < NG:
                 load_x(g + 4)
 
         g = NG - 1
         a_tanh(g - 1, 3)
         new_v(g)
+        a_unit(g, 0, 0)
         z_unit(g)
+        a_unit(g, 0, 1)
         kt = k_transposes(g - 1)
         cts = c_transposes(g - 1)
         k_copy(g - 1, kt, s_copy)
         for q, ct in enumerate(cts):
-            c_copy(g - 1, q, ct, s_copy if q == 2 else v_copy)
-        for m in range(2):
-            c_unit(g, m)
-        quant_v(g - 1, 0, 512)
-        quant_k(g - 1)
+            c_copy(g - 1, q, ct, v_copy if q == 0 else s_copy)
         a_unit(g, 1, 0)
+        a_tanh(g, 0)
         a_unit(g, 1, 1)
-        a_tanh(g, 1)
-        quant_v(g - 1, 512, 1024)
-        for q in (2, 3):
-            kv_sum(q)
+        quant_v(g - 1, 0, 1024)
+        quant_k(g - 1)
         a_unit(g, 2, 0)
+        a_tanh(g, 1)
         kt = k_transposes(g)
-        cts = c_transposes(g)
         k_copy(g, kt, s_copy)
-        c_copy(g, 0, cts[0], s_copy)
         a_unit(g, 2, 1)
         a_tanh(g, 2)
+        kvs = [(q, kv_passes(q)) for q in (2, 3)]
         for e0 in (3 * EQ, 3 * EQ + P):
             e_add_tanh(g, e0, e_passes(g, e0))
         quant_k(g)
-        quant_v(g, 0, 512)
         cuts = [(0, 512), (512, 768), (768, 896), (896, 1024)]
         kvb = {}
         for lo, hi in cuts:
@@ -515,8 +526,9 @@ def tile_flashattention_pb_t_kernel(tc, x, Wve, bve, Wxs, bxs, gamma_k_lin, beta
             for gg in range(GPB, g):
                 kv_pass(kvb[lo], lo, hi, gg)
         for lo, hi in cuts:
-            if lo:
-                quant_v(g, lo, hi)
+            quant_v(g, lo, hi)
             kv_pass(kvb[lo], lo, hi, g)
+        for q, kv in kvs:
+            kv_out(0, q * EQ, (q + 1) * EQ, kv, s_copy)
         for lo, hi in cuts:
-            kv_out(1, lo, hi, kvb[lo], v_copy if lo == 768 else s_copy)
+            kv_out(1, lo, hi, kvb[lo], v_copy if lo in (0, 768) else s_copy)

@@ -18,10 +18,11 @@ NG = B * NTOK // GROUP
 GPB = NTOK // GROUP
 EQ = 256
 NQ = E // EQ
-C_TILES = 6
+WARMING = 12
 BANKS = 8
-DVE0 = 4
-CQS = [1, 1, 1, 3, 3, 3, 2, 0]
+FIRST_BLOCKED = 4
+TURNED = [1, 1, 1, 3, 3, 3, 2, 0]
+MAX_TURNED = 2 * max(TURNED)
 
 FLOPS = 2 * B * NTOK * D * (E + S) + 2 * B * NTOK * S * E
 
@@ -34,42 +35,53 @@ def tile_flashattention_pb_t_kernel(tc, x, Wve, bve, Wxs, bxs, gamma_k_lin, beta
         xin = ctx.enter_context(tc.tile_pool(name="xin", bufs=4))
         work = ctx.enter_context(tc.tile_pool(name="work", bufs=2))
         psum = ctx.enter_context(tc.psum_pool(name="psum", bufs=1))
-        s_copy = nc.scalar.copy
-        v_copy = nc.vector.tensor_copy
-        X_ENG = [s_copy, s_copy, s_copy, s_copy]
+        on_s = nc.scalar.copy
+        on_v = nc.vector.tensor_copy
 
-        xv = x.rearrange("b (g p j) d -> (b g) p (j d)", g=GPB, p=P, j=4)
         xs, gxs, xqs, xscs = {}, {}, {}, {}
-        gvs, vqs, vscs, zts, kTs, gks, kqs, kscs, us, vTs = {}, {}, {}, {}, {}, {}, {}, {}, {}, {}
+        zts, kTs, gks, kqs, kscs = {}, {}, {}, {}, {}
+        vTs, us, gvs, vqs, vscs = {}, {}, {}, {}, {}
 
         def bank(shape, dtype, name):
             return psum.tile(shape, dtype, name=name, tag="bank", bufs=BANKS)
 
-        def load_x(g, pieces=((0, 4),)):
-            t = xin.tile([P, 4 * D], BF16, name="xs", tag="xs", align_bytes=64)
-            xs[g] = t
-            if g < DVE0:
-                for lo, hi in pieces:
-                    nc.sync.dma_start(out=t[:, lo * D : hi * D], in_=xv[g][:, lo * D : hi * D])
-                return
-            xb = x[g // GPB, (g % GPB) * GROUP : (g % GPB + 1) * GROUP, :]
+        xv = x.rearrange("b (g p j) d -> (b g) p (j d)", g=GPB, p=P, j=4)
+
+        def load_x(g, cuts=(0, 4)):
+            xs[g] = xin.tile([P, 4 * D], BF16, name="xs", tag="xs", align_bytes=64)
+            for lo, hi in zip(cuts, cuts[1:]):
+                nc.sync.dma_start(out=xs[g][:, lo * D : hi * D], in_=xv[g][:, lo * D : hi * D])
+
+        def load_x_blocks(g):
+            xs[g] = xin.tile([P, 4 * D], BF16, name="xs", tag="xs", align_bytes=64)
+            tokens = x[g // GPB, (g % GPB) * GROUP : (g % GPB + 1) * GROUP, :]
             for c in range(2):
                 for h in range(2):
                     for a in range(4):
-                        d0 = 512 * c + 256 * h + 64 * a
+                        lo = 512 * c + 256 * h + 64 * a
                         nc.sync.dma_start(
-                            out=t[32 * a + h : 32 * a + 32 : 2, c * 2 * D : (c + 1) * 2 * D].rearrange("p (k d) -> p k d", d=64),
-                            in_=xb[:, d0 : d0 + 64].rearrange("(k t) d -> t k d", t=16),
+                            out=xs[g][32 * a + h : 32 * a + 32 : 2, 2 * D * c : 2 * D * (c + 1)].rearrange(
+                                "p (k d) -> p k d", d=64
+                            ),
+                            in_=tokens[:, lo : lo + 64].rearrange("(k t) d -> t k d", t=16),
                         )
 
+        rows = const.tile([P, E + 3 * S], BF16, name="rows")
+        ones = const.tile([P, 512], BF16, name="ones")
         warm = const.tile([P, 1], F32, name="warm")
-        warm2 = const.tile([P, 1], F32, name="warm2")
-        rows = const.tile([P, E + 3 * P], BF16, name="rows")
-        ones_b = const.tile([P, P], BF16, name="ones_b")
-        nc.vector.memset(rows[:], 0.0)
+        warmed = const.tile([P, 1], F32, name="warmed")
         nc.vector.memset(warm[:], 0.0)
-        nc.vector.memset(ones_b[:], 1.0)
-        nc.scalar.activation(out=warm2[:], in_=warm[:], func=ACT.Tanh)
+        nc.vector.memset(ones[:], 1.0)
+        nc.vector.memset(rows[:], 0.0)
+        unread = bank([P, 512], F32, "unread")
+        for i in range(WARMING):
+            nc.tensor.matmul(out=unread[:], lhsT=ones[:, 0:P], rhs=ones[:], start=True, stop=True)
+        nc.scalar.activation(out=warmed[:], in_=warm[:], func=ACT.Tanh)
+        row_at = 0
+        for vec in (bve, bxs, gamma_k_lin, beta_k_lin):
+            nc.scalar.dma_start(out=rows[0:1, row_at : row_at + vec.shape[0]], in_=vec.unsqueeze(0))
+            row_at += vec.shape[0]
+
         wraw = [const.tile([P, 2, 4, E // 2], BF16, name="wraw%d" % h) for h in range(2)]
         wview = Wve.rearrange("(c u p e) n -> c u p e n", c=2, u=2, p=P, e=2)
 
@@ -78,26 +90,22 @@ def tile_flashattention_pb_t_kernel(tc, x, Wve, bve, Wxs, bxs, gamma_k_lin, beta
                 for u in range(2):
                     nc.sync.dma_start(
                         out=wraw[h][:, c, 2 * u : 2 * u + 2, :],
-                        in_=wview[c, u][:, :, h * 512 : (h + 1) * 512],
+                        in_=wview[c, u][:, :, h * (E // 2) : (h + 1) * (E // 2)],
                     )
 
-        for i, vec in enumerate((bve, bxs, gamma_k_lin, beta_k_lin)):
-            lo = 0 if i == 0 else E + (i - 1) * P
-            nc.scalar.dma_start(out=rows[0:1, lo : lo + vec.shape[0]], in_=vec.unsqueeze(0))
         load_w(0)
-        load_x(0, ((0, 1), (1, 2), (2, 4)))
+        load_x(0, cuts=(0, 1, 2, 4))
         wxraw = const.tile([P, 2, 4, S], BF16, name="wxraw")
         nc.sync.dma_start(
             out=wxraw[:].rearrange("p c (u e) n -> p (c u) (e n)", u=2),
             in_=Wxs.rearrange("(a p e) n -> p a (e n)", a=4, p=P, e=2),
         )
         load_w(1)
-        load_x(1, ((0, 2), (2, 4)))
-        for g in range(2, 4):
-            load_x(g)
-
-        ident_f = const.tile([P, P], F32, name="ident_f")
-        make_identity(nc, ident_f[:])
+        load_x(1, cuts=(0, 2, 4))
+        load_x(2)
+        load_x(3)
+        ident = const.tile([P, P], F32, name="ident")
+        make_identity(nc, ident[:])
 
         wg = const.tile([P, NQ, 2, EQ, 4], BF16, name="wg", align_bytes=64)
         wq = const.tile([P, NQ, 2, EQ], U32, name="wq", align_bytes=64)
@@ -106,14 +114,15 @@ def tile_flashattention_pb_t_kernel(tc, x, Wve, bve, Wxs, bxs, gamma_k_lin, beta
         wxq = const.tile([P, 2, S], U32, name="wxq", align_bytes=64)
         wxsc = const.tile([P, 2, S], U8, name="wxsc", align_bytes=64)
 
-        def regroup(eng_copy, dst, src):
-            eng_copy(
+        def regroup(copy, dst, src):
+            copy(
                 out=dst.rearrange("p (n i) t -> p n t i", i=4),
                 in_=src.rearrange("p t (n i) -> p n t i", i=4),
             )
 
-        def regroup_w(eng_copy, q, c):
-            regroup(eng_copy, wg[:, q, c, :, :], wraw[q // 2][:, c, :, (q % 2) * EQ : (q % 2 + 1) * EQ])
+        def regroup_w(copy, q, c):
+            lo = (q % 2) * EQ
+            regroup(copy, wg[:, q, c, :, :], wraw[q // 2][:, c, :, lo : lo + EQ])
 
         def quant_w(q):
             nc.vector.quantize_mx(
@@ -129,93 +138,90 @@ def tile_flashattention_pb_t_kernel(tc, x, Wve, bve, Wxs, bxs, gamma_k_lin, beta
                 in_=wxg[:].rearrange("p c n t -> p (c n t)"),
             )
 
-        def x_transposes(g, j):
-            xw = xs[g][:].bitcast(F32)
-            xt = bank([P, 4, P], F32, "xt")
-            for a in range(4):
-                col = j * 512 + a * P
-                nc.tensor.transpose(xt[:, a, :], xw[:, col : col + P], ident_f[:])
-            return xt
-
         def new_x(g):
             gxs[g] = work.tile([P, 4 * D], BF16, name="gx", tag="gx", align_bytes=64)
             xqs[g] = work.tile([P, 2 * GROUP], U32, name="xq", tag="xq", bufs=3, align_bytes=64)
             xscs[g] = work.tile([P, 2 * GROUP], U8, name="xsc", tag="xsc", bufs=3, align_bytes=64)
 
-        def x_blocks(g, half=None):
-            if not half:
-                new_x(g)
-            lo, hi = (0, 2 * D) if half is None else (half * D, (half + 1) * D)
-            nc.vector.transpose(out=gxs[g][:].bitcast(F32)[:, lo:hi], in_=xs[g][:].bitcast(F32)[:, lo:hi])
+        def x_column(g, c, j):
+            if g < FIRST_BLOCKED:
+                return (j // 2) * GROUP + c * 2 * P + (j % 2) * P
+            return c * GROUP + j * P
 
-        def xcol(g, c, j):
-            if g >= DVE0:
-                return c * GROUP + j * P
-            return (j // 2) * GROUP + c * 256 + (j % 2) * P
+        def x_transposes(g, j):
+            words = xs[g][:].bitcast(F32)
+            xt = bank([P, 4, P], F32, "xt")
+            for a in range(4):
+                lo = j * GROUP + a * P
+                nc.tensor.transpose(xt[:, a, :], words[:, lo : lo + P], ident[:])
+            return xt
 
-        def x_copy(g, j, xt, eng):
+        def x_copy(g, j, xt, copy):
             if j == 0:
                 new_x(g)
-            gxw = gxs[g][:].bitcast(F32).rearrange("p (a c b t u) -> p a c b t u", a=2, c=2, b=2, t=P, u=2)
-            eng(out=gxw[:, j // 2, :, j % 2, :, :], in_=xt[:].rearrange("p (c u) t -> p c t u", u=2))
+            words = gxs[g][:].bitcast(F32).rearrange("p (a c b t u) -> p a c b t u", a=2, c=2, b=2, t=P, u=2)
+            copy(out=words[:, j // 2, :, j % 2, :, :], in_=xt[:].rearrange("p (c u) t -> p c t u", u=2))
 
-        def quant_x(g, a=None):
-            lo, hi = (0, 2 * GROUP) if a is None else (a * GROUP, (a + 1) * GROUP)
+        def x_blocks(g, c):
+            if c == 0:
+                new_x(g)
+            lo, hi = c * D, (c + 1) * D
+            nc.vector.transpose(out=gxs[g][:].bitcast(F32)[:, lo:hi], in_=xs[g][:].bitcast(F32)[:, lo:hi])
+
+        def quant_x(g, half):
+            lo, hi = half * GROUP, (half + 1) * GROUP
             nc.vector.quantize_mx(
                 out=xqs[g][:, lo:hi].bitcast(FP8X4), scales=xscs[g][:, lo:hi], in_=gxs[g][:, 4 * lo : 4 * hi]
             )
 
-        def a_passes(g, q, jj):
+        def new_v(g):
+            gvs[g] = work.tile([P, E, 4], BF16, name="gv", tag="gv", align_bytes=64)
+            vqs[g] = const.tile([P, E], U32, name="vq%d" % g, align_bytes=64)
+            vscs[g] = const.tile([P, E], U8, name="vsc%d" % g, align_bytes=64)
+
+        def token_passes(g, j, dst, q, lo, hi):
+            for c in range(2):
+                at = x_column(g, c, j)
+                nc.tensor.matmul_mx(
+                    out=dst,
+                    lhsT=xqs[g][:, at : at + P].bitcast(FP8X4),
+                    lhsT_scale=xscs[g][:, at : at + P],
+                    rhs=wq[:, q, c, lo:hi].bitcast(FP8X4),
+                    rhs_scale=wsc[:, q, c, lo:hi],
+                    start=(c == 0),
+                    stop=(c == 1),
+                )
+
+        def quarter_half_passes(g, q, a):
             vb = bank([P, 2, EQ], F32, "vb")
-            for j2 in range(2):
-                for c in range(2):
-                    col = xcol(g, c, 2 * jj + j2)
-                    nc.tensor.matmul_mx(
-                        out=vb[:, j2, :],
-                        lhsT=xqs[g][:, col : col + P].bitcast(FP8X4),
-                        lhsT_scale=xscs[g][:, col : col + P],
-                        rhs=wq[:, q, c, :].bitcast(FP8X4),
-                        rhs_scale=wsc[:, q, c, :],
-                        start=(c == 0),
-                        stop=(c == 1),
-                    )
+            for b in range(2):
+                token_passes(g, 2 * a + b, vb[:, b, :], q, 0, EQ)
             return vb
 
-        def a_add(g, q, jj, vb):
-            if jj == 0:
+        def quarter_half_add(g, q, a, vb):
+            if a == 0:
                 us[(g, q)] = work.tile([P, 2, EQ, 2], F32, name="u", tag="u", bufs=4)
             nc.vector.tensor_tensor(
-                out=us[(g, q)][:, jj, :, :],
+                out=us[(g, q)][:, a, :, :],
                 in0=vb[:].rearrange("p b e -> p e b"),
                 in1=bias[:, q * EQ : (q + 1) * EQ].unsqueeze(2).to_broadcast([P, EQ, 2]),
                 op=ALU.add,
             )
 
-        def a_tanh(g, q):
+        def quarter_half(g, q, a):
+            quarter_half_add(g, q, a, quarter_half_passes(g, q, a))
+
+        def quarter_tanh(g, q):
             nc.scalar.activation(
                 out=gvs[g][:, q * EQ : (q + 1) * EQ, :].rearrange("p e (a b) -> p e a b", a=2),
                 in_=us[(g, q)][:].rearrange("p a e b -> p e a b"),
                 func=ACT.Tanh,
             )
 
-        def e_passes(g, e0):
+        def eighth(g, e0):
             vb = bank([P, 4, P], F32, "eb")
-            q, lo = e0 // EQ, e0 % EQ
             for j in range(4):
-                for c in range(2):
-                    col = xcol(g, c, j)
-                    nc.tensor.matmul_mx(
-                        out=vb[:, j, :],
-                        lhsT=xqs[g][:, col : col + P].bitcast(FP8X4),
-                        lhsT_scale=xscs[g][:, col : col + P],
-                        rhs=wq[:, q, c, lo : lo + P].bitcast(FP8X4),
-                        rhs_scale=wsc[:, q, c, lo : lo + P],
-                        start=(c == 0),
-                        stop=(c == 1),
-                    )
-            return vb
-
-        def e_add_tanh(g, e0, vb):
+                token_passes(g, j, vb[:, j, :], e0 // EQ, e0 % EQ, e0 % EQ + P)
             u = work.tile([P, P, 4], F32, name="ue", tag="ue", bufs=2)
             nc.vector.tensor_tensor(
                 out=u[:],
@@ -225,87 +231,85 @@ def tile_flashattention_pb_t_kernel(tc, x, Wve, bve, Wxs, bxs, gamma_k_lin, beta
             )
             nc.scalar.activation(out=gvs[g][:, e0 : e0 + P, :], in_=u[:], func=ACT.Tanh)
 
-        def t_passes(g, jj, cb, w, wscale):
+        def column_passes(g, a, dst, w, wscale):
             for c in range(2):
-                col = xcol(g, c, 2 * jj)
+                at = x_column(g, c, 2 * a)
                 nc.tensor.matmul_mx(
-                    out=cb[:, jj * 256 : (jj + 1) * 256],
+                    out=dst[:, a * 2 * P : (a + 1) * 2 * P],
                     lhsT=w[:, c, :].bitcast(FP8X4),
                     lhsT_scale=wscale[:, c, :],
-                    rhs=xqs[g][:, col : col + 256].bitcast(FP8X4),
-                    rhs_scale=xscs[g][:, col : col + 256],
+                    rhs=xqs[g][:, at : at + 2 * P].bitcast(FP8X4),
+                    rhs_scale=xscs[g][:, at : at + 2 * P],
                     start=(c == 0),
                     stop=(c == 1),
                 )
 
-        def t_tanh(o, cb, i):
+        def column_tanh(dst, src, i):
             nc.scalar.activation(
-                out=o[:].rearrange("p (a t b) -> p a t b", a=2, b=2),
-                in_=cb[:].rearrange("p (a b t) -> p a t b", a=2, b=2),
+                out=dst[:].rearrange("p (a t b) -> p a t b", a=2, b=2),
+                in_=src[:].rearrange("p (a b t) -> p a t b", a=2, b=2),
                 func=ACT.Tanh,
-                bias=pvec[:, i : i + 1],
+                bias=columns_bias[:, i : i + 1],
                 scale=1.0,
             )
 
-        def c_passes(g, m, jj, cb):
+        def v_tile_passes(g, m, a, cb):
             lo = (m % 2) * P
-            t_passes(g, jj, cb, wq[:, m // 2, :, lo : lo + P], wsc[:, m // 2, :, lo : lo + P])
+            column_passes(g, a, cb, wq[:, m // 2, :, lo : lo + P], wsc[:, m // 2, :, lo : lo + P])
 
-        def c_tanh(g, m, cb):
+        def v_tile_tanh(g, m, cb):
             vTs[(g, m)] = work.tile([P, GROUP], BF16, name="vT", tag="vT", bufs=8)
-            t_tanh(vTs[(g, m)], cb, 3 + m)
+            column_tanh(vTs[(g, m)], cb, 3 + m)
 
-        def c_unit(g, m):
+        def v_tile(g, m):
             cb = bank([P, GROUP], F32, "cb")
-            for jj in range(2):
-                c_passes(g, m, jj, cb)
-            c_tanh(g, m, cb)
+            for a in range(2):
+                v_tile_passes(g, m, a, cb)
+            v_tile_tanh(g, m, cb)
 
-        def z_unit(g):
-            cb = bank([P, GROUP], F32, "zb")
-            for jj in range(2):
-                t_passes(g, jj, cb, wxq, wxsc)
+        def z_tile(g):
+            zb = bank([P, GROUP], F32, "zb")
+            for a in range(2):
+                column_passes(g, a, zb, wxq, wxsc)
             zts[g] = work.tile([P, GROUP], F32, name="zt", tag="zt")
-            t_tanh(zts[g], cb, 0)
+            column_tanh(zts[g], zb, 0)
             kTs[g] = work.tile([P, GROUP], BF16, name="kT", tag="kT")
             nc.gpsimd.tensor_scalar(
-                out=kTs[g][:], in0=zts[g][:], scalar1=pvec[:, 1:2], scalar2=pvec[:, 2:3], op0=ALU.mult, op1=ALU.add
+                out=kTs[g][:],
+                in0=zts[g][:],
+                scalar1=columns_bias[:, 1:2],
+                scalar2=columns_bias[:, 2:3],
+                op0=ALU.mult,
+                op1=ALU.add,
             )
 
-        def c_quarters(g):
-            return CQS[g]
+        def turn(dst, src):
+            words = src[:].bitcast(F32)
+            for a in range(2):
+                nc.tensor.transpose(dst[:, a, :], words[:, a * P : (a + 1) * P], ident[:])
 
-        def c_transposes(g):
+        def turn_k(g):
+            kt = bank([P, 2, S], F32, "kt")
+            turn(kt, kTs[g])
+            return kt
+
+        def turn_v(g):
             cts = []
-            for q in range(c_quarters(g)):
+            for q in range(TURNED[g]):
                 ct = bank([P, 2, 2, P], F32, "ct")
                 for m in range(2):
-                    vw = vTs[(g, 2 * q + m)][:].bitcast(F32)
-                    for a in range(2):
-                        nc.tensor.transpose(ct[:, m, a, :], vw[:, a * P : (a + 1) * P], ident_f[:])
+                    turn(ct[:, m, :, :], vTs[(g, 2 * q + m)])
                 cts.append(ct)
             return cts
 
-        def c_copy(g, q, ct, eng):
-            gvw = gvs[g][:].rearrange("p e j -> p (e j)").bitcast(F32)
-            eng(
-                out=gvw[:, 2 * q * EQ : 2 * (q + 1) * EQ].rearrange("p (m e a) -> p m e a", m=2, a=2),
-                in_=ct[:].rearrange("p m a e -> p m e a"),
-            )
-
-        def k_transposes(g):
-            kt = bank([P, 2, P], F32, "kt")
-            kw = kTs[g][:].bitcast(F32)
-            for a in range(2):
-                nc.tensor.transpose(kt[:, a, :], kw[:, a * P : (a + 1) * P], ident_f[:])
-            return kt
-
-        def k_copy(g, kt, eng):
+        def k_copy(g, kt, copy):
             gks[g] = work.tile([P, S, 4], BF16, name="gk", tag="gk", align_bytes=64)
-            eng(
-                out=gks[g][:].rearrange("p s j -> p (s j)").bitcast(F32).rearrange("p (s a) -> p s a", a=2),
-                in_=kt[:].rearrange("p a s -> p s a"),
-            )
+            words = gks[g][:].rearrange("p s j -> p (s j)").bitcast(F32)
+            copy(out=words.rearrange("p (s a) -> p s a", a=2), in_=kt[:].rearrange("p a s -> p s a"))
+
+        def v_copy(g, q, ct, copy):
+            words = gvs[g][:].rearrange("p e j -> p (e j)").bitcast(F32)[:, 2 * q * EQ : 2 * (q + 1) * EQ]
+            copy(out=words.rearrange("p (m e a) -> p m e a", m=2, a=2), in_=ct[:].rearrange("p m a e -> p m e a"))
 
         def quant_v(g, lo, hi):
             nc.vector.quantize_mx(
@@ -321,7 +325,7 @@ def tile_flashattention_pb_t_kernel(tc, x, Wve, bve, Wxs, bxs, gamma_k_lin, beta
                 out=kqs[g][:].bitcast(FP8X4), scales=kscs[g][:], in_=gks[g][:].rearrange("p s j -> p (s j)")
             )
 
-        def kv_pass(kv, lo, hi, g):
+        def kv_pass(kv, g, lo, hi):
             nc.tensor.matmul_mx(
                 out=kv[:],
                 lhsT=kqs[g][:].bitcast(FP8X4),
@@ -332,203 +336,189 @@ def tile_flashattention_pb_t_kernel(tc, x, Wve, bve, Wxs, bxs, gamma_k_lin, beta
                 stop=(g % GPB == GPB - 1),
             )
 
-        def kv_passes(q):
+        def kv_store(b, lo, hi, kv, copy):
+            row = work.tile([P, hi - lo], F32, name="row", tag="row", bufs=6)
+            copy(out=row[:], in_=kv[:])
+            nc.sync.dma_start(out=out[b, :, lo:hi], in_=row[:])
+
+        def first_sum(q):
             kv = bank([P, EQ], F32, "kv")
-            for gg in range(GPB):
-                kv_pass(kv, q * EQ, (q + 1) * EQ, gg)
+            for g in range(GPB):
+                kv_pass(kv, g, q * EQ, (q + 1) * EQ)
             return kv
 
-        def kv_sum(q):
-            kv_out(0, q * EQ, (q + 1) * EQ, kv_passes(q), s_copy)
-
-        def kv_out(b, lo, hi, kv, eng):
-            osb = work.tile([P, hi - lo], F32, name="osb", tag="osb", bufs=6)
-            eng(out=osb[:], in_=kv[:])
-            nc.sync.dma_start(out=out[b, :, lo:hi], in_=osb[:])
-
-        def a_unit(g, q, jj):
-            a_add(g, q, jj, a_passes(g, q, jj))
-
-        def new_v(g):
-            gvs[g] = work.tile([P, E, 4], BF16, name="gv", tag="gv", align_bytes=64)
-            vqs[g] = const.tile([P, E], U32, name="vq%d" % g, align_bytes=64)
-            vscs[g] = const.tile([P, E], U8, name="vsc%d" % g, align_bytes=64)
-
-        regroup_w(v_copy, 0, 0)
-        regroup_w(s_copy, 1, 0)
-        regroup_w(v_copy, 0, 1)
-        regroup_w(s_copy, 1, 1)
+        regroup_w(on_v, 0, 0)
+        regroup_w(on_s, 1, 0)
+        regroup_w(on_v, 0, 1)
+        regroup_w(on_s, 1, 1)
         quant_w(0)
         new_v(0)
         xts = [x_transposes(0, j) for j in range(2)]
-        sp = bank([P, 3 + C_TILES], F32, "sp")
-        for i in range(3 + C_TILES):
-            lo = E + i * P if i < 3 else (i - 3) * P
-            nc.tensor.matmul(
-                out=sp[:, i : i + 1], lhsT=rows[:, lo : lo + P], rhs=ones_b[:, 0:1], start=True, stop=True
-            )
+        cols = bank([P, 3 + MAX_TURNED], F32, "cols")
+        for i in range(3 + MAX_TURNED):
+            lo = E + i * S if i < 3 else (i - 3) * P
+            nc.tensor.matmul(out=cols[:, i : i + 1], lhsT=rows[:, lo : lo + P], rhs=ones[:, 0:1], start=True, stop=True)
         bias = const.tile([P, E], F32, name="bias")
-        pbs = []
+        bbs = [bank([P, 512], F32, "bb") for h in range(2)]
         for h in range(2):
-            pbs.append(bank([P, 512], F32, "pb"))
-            nc.tensor.matmul(out=pbs[h][:], lhsT=ones_b[:], rhs=rows[:, h * 512 : (h + 1) * 512], start=True, stop=True)
-        x_copy(0, 0, xts[0], v_copy)
-        x_copy(0, 1, xts[1], s_copy)
+            nc.tensor.matmul(out=bbs[h][:], lhsT=ones[:, 0:P], rhs=rows[:, h * 512 : (h + 1) * 512], start=True, stop=True)
+        x_copy(0, 0, xts[0], on_v)
+        x_copy(0, 1, xts[1], on_s)
         quant_w(1)
         quant_x(0, 0)
         xts = [x_transposes(0, j) for j in range(2, 4)]
-        nc.scalar.copy(out=bias[:, 0:512], in_=pbs[0][:])
-        x_copy(0, 2, xts[0], s_copy)
-        x_copy(0, 3, xts[1], v_copy)
+        on_s(out=bias[:, 0:512], in_=bbs[0][:])
+        x_copy(0, 2, xts[0], on_s)
+        x_copy(0, 3, xts[1], on_v)
         for c in range(2):
-            regroup(v_copy, wxg[:, c, :, :], wxraw[:, c, :, :])
+            regroup(on_v, wxg[:, c, :, :], wxraw[:, c, :, :])
         quant_x(0, 1)
-        vb = a_passes(0, 1, 0)
+        vb = quarter_half_passes(0, 1, 0)
         cbs = [bank([P, GROUP], F32, "cb") for m in range(2)]
-        for jj in range(2):
+        for a in range(2):
             for m in range(2):
-                c_passes(0, m, jj, cbs[m])
-        pvec = const.tile([P, 3 + C_TILES], F32, name="pvec")
-        nc.vector.tensor_copy(out=pvec[:], in_=sp[:])
-        a_add(0, 1, 0, vb)
+                v_tile_passes(0, m, a, cbs[m])
+        columns_bias = const.tile([P, 3 + MAX_TURNED], F32, name="columns_bias")
+        on_v(out=columns_bias[:], in_=cols[:])
+        quarter_half_add(0, 1, 0, vb)
         quant_wx()
-        nc.scalar.copy(out=bias[:, 512:1024], in_=pbs[1][:])
-        regroup_w(v_copy, 2, 0)
-        regroup_w(s_copy, 3, 0)
-        regroup_w(v_copy, 2, 1)
-        regroup_w(s_copy, 3, 1)
-        a_unit(0, 1, 1)
+        on_s(out=bias[:, 512:1024], in_=bbs[1][:])
+        regroup_w(on_v, 2, 0)
+        regroup_w(on_s, 3, 0)
+        regroup_w(on_v, 2, 1)
+        regroup_w(on_s, 3, 1)
+        quarter_half(0, 1, 1)
         for m in range(2):
-            c_tanh(0, m, cbs[m])
-        z_unit(0)
+            v_tile_tanh(0, m, cbs[m])
+        z_tile(0)
         quant_w(2)
-        a_tanh(0, 1)
+        quarter_tanh(0, 1)
         xts = [x_transposes(1, j) for j in range(4)]
         quant_w(3)
-        x_copy(1, 0, xts[0], s_copy)
-        x_copy(1, 1, xts[1], v_copy)
-        a_unit(0, 2, 0)
-        x_copy(1, 2, xts[2], s_copy)
-        a_unit(0, 2, 1)
-        x_copy(1, 3, xts[3], s_copy)
+        x_copy(1, 0, xts[0], on_s)
+        x_copy(1, 1, xts[1], on_v)
+        quarter_half(0, 2, 0)
+        x_copy(1, 2, xts[2], on_s)
+        quarter_half(0, 2, 1)
+        x_copy(1, 3, xts[3], on_s)
         quant_x(1, 0)
-        a_tanh(0, 2)
-        a_unit(0, 3, 0)
+        quarter_tanh(0, 2)
+        quarter_half(0, 3, 0)
         quant_x(1, 1)
-        a_unit(0, 3, 1)
+        quarter_half(0, 3, 1)
+        load_x_blocks(4)
 
-        load_x(4)
-        for g in range(1, DVE0 - 1):
+        for g in range(1, FIRST_BLOCKED - 1):
             xts = [x_transposes(g + 1, j) for j in range(4)]
-            kt = k_transposes(g - 1)
-            cts = c_transposes(g - 1)
-            if g + 2 == DVE0:
+            kt = turn_k(g - 1)
+            cts = turn_v(g - 1)
+            if g + 2 == FIRST_BLOCKED:
                 x_blocks(g + 2, 0)
             for j in range(3):
-                x_copy(g + 1, j, xts[j], X_ENG[j])
-            a_tanh(g - 1, 3)
-            x_copy(g + 1, 3, xts[3], X_ENG[3])
-            c_copy(g - 1, 0, cts[0], v_copy)
-            k_copy(g - 1, kt, s_copy)
+                x_copy(g + 1, j, xts[j], on_s)
+            quarter_tanh(g - 1, 3)
+            x_copy(g + 1, 3, xts[3], on_s)
+            v_copy(g - 1, 0, cts[0], on_v)
+            k_copy(g - 1, kt, on_s)
             new_v(g)
-            a_unit(g, 1, 0)
+            quarter_half(g, 1, 0)
             quant_x(g + 1, 0)
-            z_unit(g)
-            a_unit(g, 1, 1)
+            z_tile(g)
+            quarter_half(g, 1, 1)
+            quarter_tanh(g, 1)
             quant_v(g - 1, 0, 512)
-            c_unit(g, 0)
-            a_tanh(g, 1)
-            a_unit(g, 2, 0)
+            v_tile(g, 0)
+            quarter_half(g, 2, 0)
             quant_k(g - 1)
             quant_x(g + 1, 1)
-            c_unit(g, 1)
-            a_unit(g, 2, 1)
+            v_tile(g, 1)
+            quarter_half(g, 2, 1)
+            quarter_tanh(g, 2)
             quant_v(g - 1, 512, 1024)
-            a_tanh(g, 2)
-            a_unit(g, 3, 0)
-            a_unit(g, 3, 1)
-            if g + 4 < NG:
-                load_x(g + 4)
-        for g in range(DVE0 - 1, NG - 1):
-            cq = c_quarters(g)
-            a_tanh(g - 1, 3)
+            quarter_half(g, 3, 0)
+            quarter_half(g, 3, 1)
+            load_x_blocks(g + 4)
+
+        def open_step(g, copies):
+            quarter_tanh(g - 1, 3)
             x_blocks(g + 1, 1)
             new_v(g)
-            z_unit(g)
-            c_unit(g, 0)
-            a_unit(g, cq, 0)
-            kt = k_transposes(g - 1)
-            cts = c_transposes(g - 1)
-            k_copy(g - 1, kt, s_copy)
+            z_tile(g)
+            v_tile(g, 0)
+            quarter_half(g, TURNED[g], 0)
+            kt = turn_k(g - 1)
+            cts = turn_v(g - 1)
+            k_copy(g - 1, kt, on_s)
             for q, ct in enumerate(cts):
-                c_copy(g - 1, q, ct, v_copy if q == 0 and cq == 3 else s_copy)
+                v_copy(g - 1, q, ct, copies[q])
             quant_x(g + 1, 0)
-            c_unit(g, 1)
-            if cq == 3:
-                c_unit(g, 2)
-                a_unit(g, 3, 1)
-            else:
-                a_unit(g, 2, 1)
-                a_tanh(g, 2)
-                c_unit(g, 2)
+            v_tile(g, 1)
+
+        for g in range(FIRST_BLOCKED - 1, NG - 2):
+            open_step(g, [on_v, on_s, on_s])
+            v_tile(g, 2)
+            quarter_half(g, 3, 1)
             quant_x(g + 1, 1)
             quant_v(g - 1, 512, 1024)
-            if cq == 3:
-                c_unit(g, 3)
-            else:
-                a_unit(g, 3, 0)
+            v_tile(g, 3)
             quant_v(g - 1, 0, 512)
             quant_k(g - 1)
             if g > GPB:
-                kv_sum(g - GPB - 1)
-            c_unit(g, 4 if cq == 3 else 3)
-            if cq == 3:
-                if g + 2 < NG:
-                    x_blocks(g + 2, 0)
-                c_unit(g, 5)
-            else:
-                a_unit(g, 3, 1)
-                if g + 2 < NG:
-                    x_blocks(g + 2, 0)
+                kv_store(0, 0, EQ, first_sum(0), on_s)
+            v_tile(g, 4)
+            x_blocks(g + 2, 0)
+            v_tile(g, 5)
             if g + 4 < NG:
-                load_x(g + 4)
+                load_x_blocks(g + 4)
+        g = NG - 2
+        open_step(g, [on_s, on_s, on_s])
+        quarter_half(g, 2, 1)
+        quarter_tanh(g, 2)
+        v_tile(g, 2)
+        quant_x(g + 1, 1)
+        quant_v(g - 1, 512, 1024)
+        quarter_half(g, 3, 0)
+        quant_v(g - 1, 0, 512)
+        quant_k(g - 1)
+        kv_store(0, EQ, 2 * EQ, first_sum(1), on_s)
+        v_tile(g, 3)
+        quarter_half(g, 3, 1)
 
         g = NG - 1
-        a_tanh(g - 1, 3)
+        quarter_tanh(g - 1, 3)
         new_v(g)
-        a_unit(g, 0, 0)
-        z_unit(g)
-        a_unit(g, 0, 1)
-        kt = k_transposes(g - 1)
-        cts = c_transposes(g - 1)
-        k_copy(g - 1, kt, s_copy)
-        for q, ct in enumerate(cts):
-            c_copy(g - 1, q, ct, v_copy if q == 0 else s_copy)
-        a_unit(g, 1, 0)
-        a_tanh(g, 0)
-        a_unit(g, 1, 1)
-        quant_v(g - 1, 0, 1024)
+        quarter_half(g, 0, 0)
+        z_tile(g)
+        quarter_half(g, 0, 1)
+        kt = turn_k(g - 1)
+        cts = turn_v(g - 1)
+        k_copy(g - 1, kt, on_s)
+        v_copy(g - 1, 0, cts[0], on_v)
+        v_copy(g - 1, 1, cts[1], on_s)
+        quarter_half(g, 1, 0)
+        quarter_tanh(g, 0)
+        quarter_half(g, 1, 1)
+        quant_v(g - 1, 0, E)
         quant_k(g - 1)
-        a_unit(g, 2, 0)
-        a_tanh(g, 1)
-        kt = k_transposes(g)
-        k_copy(g, kt, s_copy)
-        a_unit(g, 2, 1)
-        a_tanh(g, 2)
-        kvs = [(q, kv_passes(q)) for q in (2, 3)]
-        for e0 in (3 * EQ, 3 * EQ + P):
-            e_add_tanh(g, e0, e_passes(g, e0))
+        quarter_half(g, 2, 0)
+        quarter_tanh(g, 1)
+        kt = turn_k(g)
+        k_copy(g, kt, on_s)
+        quarter_half(g, 2, 1)
+        quarter_tanh(g, 2)
+        rest_of_first = [(q, first_sum(q)) for q in (2, 3)]
+        eighth(g, 3 * EQ)
+        eighth(g, 3 * EQ + P)
         quant_k(g)
         cuts = [(0, 512), (512, 768), (768, 896), (896, 1024)]
-        kvb = {}
-        for lo, hi in cuts:
-            kvb[lo] = bank([P, hi - lo], F32, "kv")
+        kvs = [bank([P, hi - lo], F32, "kv") for lo, hi in cuts]
+        for kv, (lo, hi) in zip(kvs, cuts):
             for gg in range(GPB, g):
-                kv_pass(kvb[lo], lo, hi, gg)
-        for lo, hi in cuts:
+                kv_pass(kv, gg, lo, hi)
+        for kv, (lo, hi) in zip(kvs, cuts):
             quant_v(g, lo, hi)
-            kv_pass(kvb[lo], lo, hi, g)
-        for q, kv in kvs:
-            kv_out(0, q * EQ, (q + 1) * EQ, kv, s_copy)
-        for lo, hi in cuts:
-            kv_out(1, lo, hi, kvb[lo], v_copy if lo in (0, 768) else s_copy)
+            kv_pass(kv, g, lo, hi)
+        for q, kv in rest_of_first:
+            kv_store(0, q * EQ, (q + 1) * EQ, kv, on_s)
+        for i, (kv, (lo, hi)) in enumerate(zip(kvs, cuts)):
+            kv_store(1, lo, hi, kv, on_v if i % 2 == 0 else on_s)

@@ -412,8 +412,6 @@ def tile_flashattention_pb_t_kernel(tc, x, Wve, bve, Wxs, bxs, gamma_k_lin, beta
             xts = [x_transposes(g + 1, j) for j in range(4)]
             kt = turn_k(g - 1)
             cts = turn_v(g - 1)
-            if g + 2 == FIRST_BLOCKED:
-                x_blocks(g + 2, 0)
             for j in range(3):
                 x_copy(g + 1, j, xts[j], on_s)
             quarter_tanh(g - 1, 3)
@@ -427,6 +425,8 @@ def tile_flashattention_pb_t_kernel(tc, x, Wve, bve, Wxs, bxs, gamma_k_lin, beta
             quarter_half(g, 1, 1)
             quarter_tanh(g, 1)
             quant_v(g - 1, 0, 512)
+            if g + 2 == FIRST_BLOCKED:
+                x_blocks(g + 2, 0)
             v_tile(g, 0)
             quarter_half(g, 2, 0)
             quant_k(g - 1)
@@ -498,12 +498,13 @@ def tile_flashattention_pb_t_kernel(tc, x, Wve, bve, Wxs, bxs, gamma_k_lin, beta
         quarter_half(g, 1, 0)
         quarter_tanh(g, 0)
         quarter_half(g, 1, 1)
-        quant_v(g - 1, 0, E)
+        quant_v(g - 1, 0, 512)
         quant_k(g - 1)
         quarter_half(g, 2, 0)
         quarter_tanh(g, 1)
         kt = turn_k(g)
         k_copy(g, kt, on_s)
+        quant_v(g - 1, 512, 1024)
         quarter_half(g, 2, 1)
         quarter_tanh(g, 2)
         rest_of_first = [(q, first_sum(q)) for q in (2, 3)]

@@ -386,10 +386,10 @@ def tile_flashattention_pb_t_kernel(tc, x, Wve, bve, Wxs, bxs, gamma_k_lin, beta
         regroup_w(on_v, 2, 0)
         regroup_w(on_s, 3, 0)
         regroup_w(on_v, 2, 1)
-        regroup_w(on_s, 3, 1)
         quarter_half(0, 1, 1)
         for m in range(2):
             v_tile_tanh(0, m, cbs[m])
+        regroup_w(on_s, 3, 1)
         z_tile(0)
         quant_w(2)
         quarter_tanh(0, 1)
@@ -434,9 +434,9 @@ def tile_flashattention_pb_t_kernel(tc, x, Wve, bve, Wxs, bxs, gamma_k_lin, beta
             v_tile(g, 1)
             quarter_half(g, 2, 1)
             quarter_tanh(g, 2)
-            quant_v(g - 1, 512, 1024)
             quarter_half(g, 3, 0)
             quarter_half(g, 3, 1)
+            quant_v(g - 1, 512, 1024)
             load_x_blocks(g + 4)
 
         def open_step(g, copies):
@@ -457,8 +457,8 @@ def tile_flashattention_pb_t_kernel(tc, x, Wve, bve, Wxs, bxs, gamma_k_lin, beta
         for g in range(FIRST_BLOCKED - 1, NG - 2):
             open_step(g, [on_v, on_s, on_s])
             v_tile(g, 2)
-            quarter_half(g, 3, 1)
             quant_x(g + 1, 1)
+            quarter_half(g, 3, 1)
             quant_v(g - 1, 512, 1024)
             v_tile(g, 3)
             quant_v(g - 1, 0, 512)
@@ -485,10 +485,10 @@ def tile_flashattention_pb_t_kernel(tc, x, Wve, bve, Wxs, bxs, gamma_k_lin, beta
         quarter_half(g, 3, 1)
 
         g = NG - 1
-        quarter_tanh(g - 1, 3)
         new_v(g)
         quarter_half(g, 0, 0)
         z_tile(g)
+        quarter_tanh(g - 1, 3)
         quarter_half(g, 0, 1)
         kt = turn_k(g - 1)
         cts = turn_v(g - 1)

@@ -18,7 +18,7 @@ NG = B * NTOK // GROUP
 GPB = NTOK // GROUP
 EQ = 256
 NQ = E // EQ
-WARMING = 12
+WARMING = 20
 BANKS = 8
 FIRST_BLOCKED = 4
 TURNED = [1, 1, 1, 3, 3, 3, 2, 0]
@@ -73,9 +73,12 @@ def tile_flashattention_pb_t_kernel(tc, x, Wve, bve, Wxs, bxs, gamma_k_lin, beta
         nc.vector.memset(warm[:], 0.0)
         nc.vector.memset(ones[:], 1.0)
         nc.vector.memset(rows[:], 0.0)
-        unread = bank([P, 512], F32, "unread")
-        for i in range(WARMING):
-            nc.tensor.matmul(out=unread[:], lhsT=ones[:, 0:P], rhs=ones[:], start=True, stop=True)
+        def keep_clock(n):
+            unread = bank([P, 512], F32, "unread")
+            for i in range(n):
+                nc.tensor.matmul(out=unread[:], lhsT=ones[:, 0:P], rhs=ones[:], start=True, stop=True)
+
+        keep_clock(WARMING)
         nc.scalar.activation(out=warmed[:], in_=warm[:], func=ACT.Tanh)
         row_at = 0
         for vec in (bve, bxs, gamma_k_lin, beta_k_lin):
@@ -354,6 +357,7 @@ def tile_flashattention_pb_t_kernel(tc, x, Wve, bve, Wxs, bxs, gamma_k_lin, beta
         quant_w(0)
         new_v(0)
         xts = [x_transposes(0, j) for j in range(2)]
+        keep_clock(1)
         cols = bank([P, 3 + MAX_TURNED], F32, "cols")
         for i in range(3 + MAX_TURNED):
             lo = E + i * S if i < 3 else (i - 3) * P
@@ -367,6 +371,7 @@ def tile_flashattention_pb_t_kernel(tc, x, Wve, bve, Wxs, bxs, gamma_k_lin, beta
         quant_w(1)
         quant_x(0, 0)
         xts = [x_transposes(0, j) for j in range(2, 4)]
+        keep_clock(2)
         on_s(out=bias[:, 0:512], in_=bbs[0][:])
         x_copy(0, 2, xts[0], on_s)
         x_copy(0, 3, xts[1], on_v)
@@ -393,7 +398,10 @@ def tile_flashattention_pb_t_kernel(tc, x, Wve, bve, Wxs, bxs, gamma_k_lin, beta
         z_tile(0)
         quant_w(2)
         quarter_tanh(0, 1)
-        xts = [x_transposes(1, j) for j in range(4)]
+        keep_clock(1)
+        xts = [x_transposes(1, j) for j in range(2)]
+        keep_clock(1)
+        xts += [x_transposes(1, j) for j in range(2, 4)]
         quant_w(3)
         x_copy(1, 0, xts[0], on_s)
         x_copy(1, 1, xts[1], on_v)
@@ -405,17 +413,19 @@ def tile_flashattention_pb_t_kernel(tc, x, Wve, bve, Wxs, bxs, gamma_k_lin, beta
         quarter_tanh(0, 2)
         quarter_half(0, 3, 0)
         quant_x(1, 1)
+        xts = [x_transposes(2, j) for j in range(2)]
+        for j in range(2):
+            x_copy(2, j, xts[j], on_s)
         quarter_half(0, 3, 1)
         load_x_blocks(4)
 
         for g in range(1, FIRST_BLOCKED - 1):
-            xts = [x_transposes(g + 1, j) for j in range(4)]
+            xts = [x_transposes(g + 1, j) for j in range(2, 4)]
             kt = turn_k(g - 1)
             cts = turn_v(g - 1)
-            for j in range(3):
-                x_copy(g + 1, j, xts[j], on_s)
+            x_copy(g + 1, 2, xts[0], on_s)
             quarter_tanh(g - 1, 3)
-            x_copy(g + 1, 3, xts[3], on_s)
+            x_copy(g + 1, 3, xts[1], on_s)
             v_copy(g - 1, 0, cts[0], on_v)
             k_copy(g - 1, kt, on_s)
             new_v(g)
@@ -429,6 +439,10 @@ def tile_flashattention_pb_t_kernel(tc, x, Wve, bve, Wxs, bxs, gamma_k_lin, beta
                 x_blocks(g + 2, 0)
             v_tile(g, 0)
             quarter_half(g, 2, 0)
+            if g + 2 < FIRST_BLOCKED:
+                xts = [x_transposes(g + 2, j) for j in range(2)]
+                for j in range(2):
+                    x_copy(g + 2, j, xts[j], on_s)
             quant_k(g - 1)
             quant_x(g + 1, 1)
             v_tile(g, 1)

@@ -18,7 +18,7 @@ NG = B * NTOK // GROUP
 GPB = NTOK // GROUP
 EQ = 256
 NQ = E // EQ
-WARMING = 20
+WARMING = 12
 BANKS = 8
 FIRST_BLOCKED = 4
 TURNED = [1, 1, 1, 3, 3, 3, 2, 0]
@@ -362,17 +362,18 @@ def tile_flashattention_pb_t_kernel(tc, x, Wve, bve, Wxs, bxs, gamma_k_lin, beta
         for i in range(3 + MAX_TURNED):
             lo = E + i * S if i < 3 else (i - 3) * P
             nc.tensor.matmul(out=cols[:, i : i + 1], lhsT=rows[:, lo : lo + P], rhs=ones[:, 0:1], start=True, stop=True)
-        bias = const.tile([P, E], F32, name="bias")
-        bbs = [bank([P, 512], F32, "bb") for h in range(2)]
+        bias = const.tile([P, E], BF16, name="bias")
+        bb = bank([P, E], BF16, "bb")
         for h in range(2):
-            nc.tensor.matmul(out=bbs[h][:], lhsT=ones[:, 0:P], rhs=rows[:, h * 512 : (h + 1) * 512], start=True, stop=True)
+            cut = slice(h * 512, (h + 1) * 512)
+            nc.tensor.matmul(out=bb[:, cut], lhsT=ones[:, 0:P], rhs=rows[:, cut], start=True, stop=True)
         x_copy(0, 0, xts[0], on_v)
         x_copy(0, 1, xts[1], on_s)
         quant_w(1)
         quant_x(0, 0)
         xts = [x_transposes(0, j) for j in range(2, 4)]
         keep_clock(2)
-        on_s(out=bias[:, 0:512], in_=bbs[0][:])
+        on_s(out=bias[:], in_=bb[:])
         x_copy(0, 2, xts[0], on_s)
         x_copy(0, 3, xts[1], on_v)
         for c in range(2):
@@ -387,7 +388,6 @@ def tile_flashattention_pb_t_kernel(tc, x, Wve, bve, Wxs, bxs, gamma_k_lin, beta
         on_v(out=columns_bias[:], in_=cols[:])
         quarter_half_add(0, 1, 0, vb)
         quant_wx()
-        on_s(out=bias[:, 512:1024], in_=bbs[1][:])
         regroup_w(on_v, 2, 0)
         regroup_w(on_s, 3, 0)
         regroup_w(on_v, 2, 1)
@@ -513,13 +513,13 @@ def tile_flashattention_pb_t_kernel(tc, x, Wve, bve, Wxs, bxs, gamma_k_lin, beta
         quarter_tanh(g, 0)
         quarter_half(g, 1, 1)
         quant_v(g - 1, 0, 512)
-        quant_k(g - 1)
         quarter_half(g, 2, 0)
         quarter_tanh(g, 1)
         kt = turn_k(g)
         k_copy(g, kt, on_s)
-        quant_v(g - 1, 512, 1024)
         quarter_half(g, 2, 1)
+        quant_k(g - 1)
+        quant_v(g - 1, 512, 1024)
         quarter_tanh(g, 2)
         rest_of_first = [(q, first_sum(q)) for q in (2, 3)]
         eighth(g, 3 * EQ)

@@ -234,15 +234,19 @@ def tile_flashattention_pb_t_kernel(tc, x, Wve, bve, Wxs, bxs, gamma_k_lin, beta
             )
             nc.scalar.activation(out=gvs[g][:, e0 : e0 + P, :], in_=u[:], func=ACT.Tanh)
 
+        def column_pieces(g):
+            return 2 if g < FIRST_BLOCKED else 1
+
         def column_passes(g, a, dst, w, wscale):
+            n = GROUP // column_pieces(g)
             for c in range(2):
-                at = x_column(g, c, 2 * a)
+                at = x_column(g, c, a * n // P)
                 nc.tensor.matmul_mx(
-                    out=dst[:, a * 2 * P : (a + 1) * 2 * P],
+                    out=dst[:, a * n : (a + 1) * n],
                     lhsT=w[:, c, :].bitcast(FP8X4),
                     lhsT_scale=wscale[:, c, :],
-                    rhs=xqs[g][:, at : at + 2 * P].bitcast(FP8X4),
-                    rhs_scale=xscs[g][:, at : at + 2 * P],
+                    rhs=xqs[g][:, at : at + n].bitcast(FP8X4),
+                    rhs_scale=xscs[g][:, at : at + n],
                     start=(c == 0),
                     stop=(c == 1),
                 )
@@ -266,13 +270,13 @@ def tile_flashattention_pb_t_kernel(tc, x, Wve, bve, Wxs, bxs, gamma_k_lin, beta
 
         def v_tile(g, m):
             cb = bank([P, GROUP], F32, "cb")
-            for a in range(2):
+            for a in range(column_pieces(g)):
                 v_tile_passes(g, m, a, cb)
             v_tile_tanh(g, m, cb)
 
         def z_tile(g):
             zb = bank([P, GROUP], F32, "zb")
-            for a in range(2):
+            for a in range(column_pieces(g)):
                 column_passes(g, a, zb, wxq, wxsc)
             zts[g] = work.tile([P, GROUP], F32, name="zt", tag="zt")
             column_tanh(zts[g], zb, 0)
@@ -356,8 +360,15 @@ def tile_flashattention_pb_t_kernel(tc, x, Wve, bve, Wxs, bxs, gamma_k_lin, beta
         regroup_w(on_s, 1, 1)
         quant_w(0)
         new_v(0)
-        xts = [x_transposes(0, j) for j in range(2)]
+        xts = [x_transposes(0, 0)]
         keep_clock(1)
+        xts.append(x_transposes(0, 1))
+        keep_clock(2)
+        x_copy(0, 0, xts[0], on_v)
+        x_copy(0, 1, xts[1], on_s)
+        quant_w(1)
+        quant_x(0, 0)
+        xts = [x_transposes(0, j) for j in range(2, 4)]
         cols = bank([P, 3 + MAX_TURNED], F32, "cols")
         for i in range(3 + MAX_TURNED):
             lo = E + i * S if i < 3 else (i - 3) * P
@@ -367,18 +378,12 @@ def tile_flashattention_pb_t_kernel(tc, x, Wve, bve, Wxs, bxs, gamma_k_lin, beta
         for h in range(2):
             cut = slice(h * 512, (h + 1) * 512)
             nc.tensor.matmul(out=bb[:, cut], lhsT=ones[:, 0:P], rhs=rows[:, cut], start=True, stop=True)
-        x_copy(0, 0, xts[0], on_v)
-        x_copy(0, 1, xts[1], on_s)
-        quant_w(1)
-        quant_x(0, 0)
-        xts = [x_transposes(0, j) for j in range(2, 4)]
-        keep_clock(2)
-        on_s(out=bias[:], in_=bb[:])
         x_copy(0, 2, xts[0], on_s)
         x_copy(0, 3, xts[1], on_v)
         for c in range(2):
             regroup(on_v, wxg[:, c, :, :], wxraw[:, c, :, :])
         quant_x(0, 1)
+        on_s(out=bias[:], in_=bb[:])
         vb = quarter_half_passes(0, 1, 0)
         cbs = [bank([P, GROUP], F32, "cb") for m in range(2)]
         for a in range(2):
@@ -521,9 +526,9 @@ def tile_flashattention_pb_t_kernel(tc, x, Wve, bve, Wxs, bxs, gamma_k_lin, beta
         quant_k(g - 1)
         quant_v(g - 1, 512, 1024)
         quarter_tanh(g, 2)
-        rest_of_first = [(q, first_sum(q)) for q in (2, 3)]
         eighth(g, 3 * EQ)
         eighth(g, 3 * EQ + P)
+        rest_of_first = [(q, first_sum(q)) for q in (2, 3)]
         quant_k(g)
         cuts = [(0, 512), (512, 768), (768, 896), (896, 1024)]
         kvs = [bank([P, hi - lo], F32, "kv") for lo, hi in cuts]

@@ -111,11 +111,11 @@ def tile_flashattention_pb_t_kernel(tc, x, Wve, bve, Wxs, bxs, gamma_k_lin, beta
         make_identity(nc, ident[:])
 
         wg = const.tile([P, NQ, 2, EQ, 4], BF16, name="wg", align_bytes=64)
-        wq = const.tile([P, NQ, 2, EQ], U32, name="wq", align_bytes=64)
-        wsc = const.tile([P, NQ, 2, EQ], U8, name="wsc", align_bytes=64)
+        wq = const.tile([P, NQ, 2, EQ], U32, name="wq", align_bytes=256)
+        wsc = const.tile([P, NQ, 2, EQ], U8, name="wsc", align_bytes=256)
         wxg = const.tile([P, 2, S, 4], BF16, name="wxg", align_bytes=64)
-        wxq = const.tile([P, 2, S], U32, name="wxq", align_bytes=64)
-        wxsc = const.tile([P, 2, S], U8, name="wxsc", align_bytes=64)
+        wxq = const.tile([P, 2, S], U32, name="wxq", align_bytes=256)
+        wxsc = const.tile([P, 2, S], U8, name="wxsc", align_bytes=256)
 
         def regroup(copy, dst, src):
             copy(
@@ -143,8 +143,8 @@ def tile_flashattention_pb_t_kernel(tc, x, Wve, bve, Wxs, bxs, gamma_k_lin, beta
 
         def new_x(g):
             gxs[g] = work.tile([P, 4 * D], BF16, name="gx", tag="gx", align_bytes=64)
-            xqs[g] = work.tile([P, 2 * GROUP], U32, name="xq", tag="xq", bufs=3, align_bytes=64)
-            xscs[g] = work.tile([P, 2 * GROUP], U8, name="xsc", tag="xsc", bufs=3, align_bytes=64)
+            xqs[g] = work.tile([P, 2 * GROUP], U32, name="xq", tag="xq", bufs=3, align_bytes=256)
+            xscs[g] = work.tile([P, 2 * GROUP], U8, name="xsc", tag="xsc", bufs=3, align_bytes=256)
 
         def x_column(g, c, j):
             if g < FIRST_BLOCKED:
@@ -179,8 +179,8 @@ def tile_flashattention_pb_t_kernel(tc, x, Wve, bve, Wxs, bxs, gamma_k_lin, beta
 
         def new_v(g):
             gvs[g] = work.tile([P, E, 4], BF16, name="gv", tag="gv", align_bytes=64)
-            vqs[g] = const.tile([P, E], U32, name="vq%d" % g, align_bytes=64)
-            vscs[g] = const.tile([P, E], U8, name="vsc%d" % g, align_bytes=64)
+            vqs[g] = const.tile([P, E], U32, name="vq%d" % g, align_bytes=256)
+            vscs[g] = const.tile([P, E], U8, name="vsc%d" % g, align_bytes=256)
 
         def token_passes(g, j, dst, q, lo, hi):
             for c in range(2):
@@ -326,8 +326,8 @@ def tile_flashattention_pb_t_kernel(tc, x, Wve, bve, Wxs, bxs, gamma_k_lin, beta
             )
 
         def quant_k(g):
-            kqs[g] = const.tile([P, S], U32, name="kq%d" % g, align_bytes=64)
-            kscs[g] = const.tile([P, S], U8, name="ksc%d" % g, align_bytes=64)
+            kqs[g] = const.tile([P, S], U32, name="kq%d" % g, align_bytes=256)
+            kscs[g] = const.tile([P, S], U8, name="ksc%d" % g, align_bytes=256)
             nc.vector.quantize_mx(
                 out=kqs[g][:].bitcast(FP8X4), scales=kscs[g][:], in_=gks[g][:].rearrange("p s j -> p (s j)")
             )

@@ -384,43 +384,41 @@ def tile_flashattention_pb_t_kernel(tc, x, Wve, bve, Wxs, bxs, gamma_k_lin, beta
             regroup(on_v, wxg[:, c, :, :], wxraw[:, c, :, :])
         quant_x(0, 1)
         on_s(out=bias[:], in_=bb[:])
-        vb = quarter_half_passes(0, 1, 0)
+        vbs = [quarter_half_passes(0, 1, 0)]
         cbs = [bank([P, GROUP], F32, "cb") for m in range(2)]
         for a in range(2):
             for m in range(2):
                 v_tile_passes(0, m, a, cbs[m])
         columns_bias = const.tile([P, 3 + MAX_TURNED], F32, name="columns_bias")
         on_v(out=columns_bias[:], in_=cols[:])
-        quarter_half_add(0, 1, 0, vb)
         quant_wx()
-        regroup_w(on_v, 2, 0)
-        regroup_w(on_s, 3, 0)
-        regroup_w(on_v, 2, 1)
-        quarter_half(0, 1, 1)
+        for c in range(2):
+            regroup_w(on_v, 2, c)
+            regroup_w(on_s, 3, c)
+        vbs.append(quarter_half_passes(0, 1, 1))
+        quarter_half_add(0, 1, 0, vbs[0])
+        quant_w(2)
         for m in range(2):
             v_tile_tanh(0, m, cbs[m])
-        regroup_w(on_s, 3, 1)
         z_tile(0)
-        quant_w(2)
-        quarter_tanh(0, 1)
-        keep_clock(1)
-        xts = [x_transposes(1, j) for j in range(2)]
-        keep_clock(1)
-        xts += [x_transposes(1, j) for j in range(2, 4)]
+        quarter_half_add(0, 1, 1, vbs[1])
         quant_w(3)
+        xts = [x_transposes(1, j) for j in range(2)]
+        quarter_half(0, 2, 0)
         x_copy(1, 0, xts[0], on_s)
         x_copy(1, 1, xts[1], on_v)
-        quarter_half(0, 2, 0)
-        x_copy(1, 2, xts[2], on_s)
+        quarter_tanh(0, 1)
         quarter_half(0, 2, 1)
-        x_copy(1, 3, xts[3], on_s)
+        xts = [x_transposes(1, j) for j in range(2, 4)]
+        x_copy(1, 2, xts[0], on_s)
         quant_x(1, 0)
-        quarter_tanh(0, 2)
+        x_copy(1, 3, xts[1], on_s)
         quarter_half(0, 3, 0)
+        quarter_tanh(0, 2)
         quant_x(1, 1)
         xts = [x_transposes(2, j) for j in range(2)]
-        for j in range(2):
-            x_copy(2, j, xts[j], on_s)
+        x_copy(2, 0, xts[0], on_v)
+        x_copy(2, 1, xts[1], on_s)
         quarter_half(0, 3, 1)
         load_x_blocks(4)
 

from contextlib import ExitStack

import concourse.mybir as mybir
from concourse.masks import make_identity

F32 = mybir.dt.float32
BF16 = mybir.dt.bfloat16
U32 = mybir.dt.uint32
U8 = mybir.dt.uint8
FP8X4 = mybir.dt.float8_e4m3fn_x4
ACT = mybir.ActivationFunctionType
ALU = mybir.AluOpType

P = 128
B, NTOK, D, E, S = 2, 2048, 1024, 1024, 128
GROUP = 512
NG = B * NTOK // GROUP
GPB = NTOK // GROUP
EQ = 256
NQ = E // EQ
WARMING = 12
BANKS = 8
FIRST_BLOCKED = 4
TURNED = [1, 1, 1, 3, 3, 3, 2, 0]
MAX_TURNED = 2 * max(TURNED)

FLOPS = 2 * B * NTOK * D * (E + S) + 2 * B * NTOK * S * E


def tile_flashattention_pb_t_kernel(tc, x, Wve, bve, Wxs, bxs, gamma_k_lin, beta_k_lin, out):
    nc = tc.nc
    with ExitStack() as ctx:
        ctx.enter_context(tc.manual_schedule())
        const = ctx.enter_context(tc.tile_pool(name="const", bufs=1))
        xin = ctx.enter_context(tc.tile_pool(name="xin", bufs=4))
        work = ctx.enter_context(tc.tile_pool(name="work", bufs=2))
        psum = ctx.enter_context(tc.psum_pool(name="psum", bufs=1))
        on_s = nc.scalar.copy
        on_v = nc.vector.tensor_copy

        xs, gxs, xqs, xscs = {}, {}, {}, {}
        zts, kTs, gks, kqs, kscs = {}, {}, {}, {}, {}
        vTs, us, gvs, vqs, vscs = {}, {}, {}, {}, {}

        def bank(shape, dtype, name):
            return psum.tile(shape, dtype, name=name, tag="bank", bufs=BANKS)

        xv = x.rearrange("b (g p j) d -> (b g) p (j d)", g=GPB, p=P, j=4)

        def load_x(g, cuts=(0, 4)):
            xs[g] = xin.tile([P, 4 * D], BF16, name="xs", tag="xs", align_bytes=64)
            for lo, hi in zip(cuts, cuts[1:]):
                nc.sync.dma_start(out=xs[g][:, lo * D : hi * D], in_=xv[g][:, lo * D : hi * D])

        def load_x_blocks(g):
            xs[g] = xin.tile([P, 4 * D], BF16, name="xs", tag="xs", align_bytes=64)
            tokens = x[g // GPB, (g % GPB) * GROUP : (g % GPB + 1) * GROUP, :]
            for c in range(2):
                for h in range(2):
                    for a in range(4):
                        lo = 512 * c + 256 * h + 64 * a
                        nc.sync.dma_start(
                            out=xs[g][32 * a + h : 32 * a + 32 : 2, 2 * D * c : 2 * D * (c + 1)].rearrange(
                                "p (k d) -> p k d", d=64
                            ),
                            in_=tokens[:, lo : lo + 64].rearrange("(k t) d -> t k d", t=16),
                        )

        rows = const.tile([P, E + 3 * S], BF16, name="rows")
        ones = const.tile([P, 512], BF16, name="ones")
        warm = const.tile([P, 1], F32, name="warm")
        warmed = const.tile([P, 1], F32, name="warmed")
        nc.vector.memset(warm[:], 0.0)
        nc.vector.memset(ones[:], 1.0)
        nc.vector.memset(rows[:], 0.0)
        def keep_clock(n):
            unread = bank([P, 512], F32, "unread")
            for i in range(n):
                nc.tensor.matmul(out=unread[:], lhsT=ones[:, 0:P], rhs=ones[:], start=True, stop=True)

        keep_clock(WARMING)
        nc.scalar.activation(out=warmed[:], in_=warm[:], func=ACT.Tanh)
        row_at = 0
        for vec in (bve, bxs, gamma_k_lin, beta_k_lin):
            nc.scalar.dma_start(out=rows[0:1, row_at : row_at + vec.shape[0]], in_=vec.unsqueeze(0))
            row_at += vec.shape[0]

        wraw = [const.tile([P, 2, 4, E // 2], BF16, name="wraw%d" % h) for h in range(2)]
        wview = Wve.rearrange("(c u p e) n -> c u p e n", c=2, u=2, p=P, e=2)

        def load_w(h):
            for c in range(2):
                for u in range(2):
                    nc.sync.dma_start(
                        out=wraw[h][:, c, 2 * u : 2 * u + 2, :],
                        in_=wview[c, u][:, :, h * (E // 2) : (h + 1) * (E // 2)],
                    )

        load_w(0)
        load_x(0, cuts=(0, 1, 2, 4))
        wxraw = const.tile([P, 2, 4, S], BF16, name="wxraw")
        nc.sync.dma_start(
            out=wxraw[:].rearrange("p c (u e) n -> p (c u) (e n)", u=2),
            in_=Wxs.rearrange("(a p e) n -> p a (e n)", a=4, p=P, e=2),
        )
        load_w(1)
        load_x(1, cuts=(0, 2, 4))
        load_x(2)
        load_x(3)
        ident = const.tile([P, P], F32, name="ident")
        make_identity(nc, ident[:])

        wg = const.tile([P, NQ, 2, EQ, 4], BF16, name="wg", align_bytes=64)
        wq = const.tile([P, NQ, 2, EQ], U32, name="wq", align_bytes=256)
        wsc = const.tile([P, NQ, 2, EQ], U8, name="wsc", align_bytes=256)
        wxg = const.tile([P, 2, S, 4], BF16, name="wxg", align_bytes=64)
        wxq = const.tile([P, 2, S], U32, name="wxq", align_bytes=256)
        wxsc = const.tile([P, 2, S], U8, name="wxsc", align_bytes=256)

        def regroup(copy, dst, src):
            copy(
                out=dst.rearrange("p (n i) t -> p n t i", i=4),
                in_=src.rearrange("p t (n i) -> p n t i", i=4),
            )

        def regroup_w(copy, q, c):
            lo = (q % 2) * EQ
            regroup(copy, wg[:, q, c, :, :], wraw[q // 2][:, c, :, lo : lo + EQ])

        def quant_w(q):
            nc.vector.quantize_mx(
                out=wq[:, q, :, :].rearrange("p c n -> p (c n)").bitcast(FP8X4),
                scales=wsc[:, q, :, :].rearrange("p c n -> p (c n)"),
                in_=wg[:, q, :, :, :].rearrange("p c n t -> p (c n t)"),
            )

        def quant_wx():
            nc.vector.quantize_mx(
                out=wxq[:].rearrange("p c n -> p (c n)").bitcast(FP8X4),
                scales=wxsc[:].rearrange("p c n -> p (c n)"),
                in_=wxg[:].rearrange("p c n t -> p (c n t)"),
            )

        def new_x(g):
            gxs[g] = work.tile([P, 4 * D], BF16, name="gx", tag="gx", align_bytes=64)
            xqs[g] = work.tile([P, 2 * GROUP], U32, name="xq", tag="xq", bufs=3, align_bytes=256)
            xscs[g] = work.tile([P, 2 * GROUP], U8, name="xsc", tag="xsc", bufs=3, align_bytes=256)

        def x_column(g, c, j):
            if g < FIRST_BLOCKED:
                return (j // 2) * GROUP + c * 2 * P + (j % 2) * P
            return c * GROUP + j * P

        def x_transposes(g, j):
            words = xs[g][:].bitcast(F32)
            xt = bank([P, 4, P], F32, "xt")
            for a in range(4):
                lo = j * GROUP + a * P
                nc.tensor.transpose(xt[:, a, :], words[:, lo : lo + P], ident[:])
            return xt

        def x_copy(g, j, xt, copy):
            if j == 0:
                new_x(g)
            words = gxs[g][:].bitcast(F32).rearrange("p (a c b t u) -> p a c b t u", a=2, c=2, b=2, t=P, u=2)
            copy(out=words[:, j // 2, :, j % 2, :, :], in_=xt[:].rearrange("p (c u) t -> p c t u", u=2))

        def x_blocks(g, c):
            if c == 0:
                new_x(g)
            lo, hi = c * D, (c + 1) * D
            nc.vector.transpose(out=gxs[g][:].bitcast(F32)[:, lo:hi], in_=xs[g][:].bitcast(F32)[:, lo:hi])

        def quant_x(g, half):
            lo, hi = half * GROUP, (half + 1) * GROUP
            nc.vector.quantize_mx(
                out=xqs[g][:, lo:hi].bitcast(FP8X4), scales=xscs[g][:, lo:hi], in_=gxs[g][:, 4 * lo : 4 * hi]
            )

        def new_v(g):
            gvs[g] = work.tile([P, E, 4], BF16, name="gv", tag="gv", align_bytes=64)
            vqs[g] = const.tile([P, E], U32, name="vq%d" % g, align_bytes=256)
            vscs[g] = const.tile([P, E], U8, name="vsc%d" % g, align_bytes=256)

        def token_passes(g, j, dst, q, lo, hi):
            for c in range(2):
                at = x_column(g, c, j)
                nc.tensor.matmul_mx(
                    out=dst,
                    lhsT=xqs[g][:, at : at + P].bitcast(FP8X4),
                    lhsT_scale=xscs[g][:, at : at + P],
                    rhs=wq[:, q, c, lo:hi].bitcast(FP8X4),
                    rhs_scale=wsc[:, q, c, lo:hi],
                    start=(c == 0),
                    stop=(c == 1),
                )

        def quarter_half_passes(g, q, a):
            vb = bank([P, 2, EQ], F32, "vb")
            for b in range(2):
                token_passes(g, 2 * a + b, vb[:, b, :], q, 0, EQ)
            return vb

        def quarter_half_add(g, q, a, vb):
            if a == 0:
                us[(g, q)] = work.tile([P, 2, EQ, 2], F32, name="u", tag="u", bufs=4)
            nc.vector.tensor_tensor(
                out=us[(g, q)][:, a, :, :],
                in0=vb[:].rearrange("p b e -> p e b"),
                in1=bias[:, q * EQ : (q + 1) * EQ].unsqueeze(2).to_broadcast([P, EQ, 2]),
                op=ALU.add,
            )

        def quarter_half(g, q, a):
            quarter_half_add(g, q, a, quarter_half_passes(g, q, a))

        def quarter_tanh(g, q):
            nc.scalar.activation(
                out=gvs[g][:, q * EQ : (q + 1) * EQ, :].rearrange("p e (a b) -> p e a b", a=2),
                in_=us[(g, q)][:].rearrange("p a e b -> p e a b"),
                func=ACT.Tanh,
            )

        def eighth(g, e0):
            vb = bank([P, 4, P], F32, "eb")
            for j in range(4):
                token_passes(g, j, vb[:, j, :], e0 // EQ, e0 % EQ, e0 % EQ + P)
            u = work.tile([P, P, 4], F32, name="ue", tag="ue", bufs=2)
            nc.vector.tensor_tensor(
                out=u[:],
                in0=vb[:].rearrange("p j e -> p e j"),
                in1=bias[:, e0 : e0 + P].unsqueeze(2).to_broadcast([P, P, 4]),
                op=ALU.add,
            )
            nc.scalar.activation(out=gvs[g][:, e0 : e0 + P, :], in_=u[:], func=ACT.Tanh)

        def column_pieces(g):
            return 2 if g < FIRST_BLOCKED else 1

        def column_passes(g, a, dst, w, wscale):
            n = GROUP // column_pieces(g)
            for c in range(2):
                at = x_column(g, c, a * n // P)
                nc.tensor.matmul_mx(
                    out=dst[:, a * n : (a + 1) * n],
                    lhsT=w[:, c, :].bitcast(FP8X4),
                    lhsT_scale=wscale[:, c, :],
                    rhs=xqs[g][:, at : at + n].bitcast(FP8X4),
                    rhs_scale=xscs[g][:, at : at + n],
                    start=(c == 0),
                    stop=(c == 1),
                )

        def column_tanh(dst, src, i):
            nc.scalar.activation(
                out=dst[:].rearrange("p (a t b) -> p a t b", a=2, b=2),
                in_=src[:].rearrange("p (a b t) -> p a t b", a=2, b=2),
                func=ACT.Tanh,
                bias=columns_bias[:, i : i + 1],
                scale=1.0,
            )

        def v_tile_passes(g, m, a, cb):
            lo = (m % 2) * P
            column_passes(g, a, cb, wq[:, m // 2, :, lo : lo + P], wsc[:, m // 2, :, lo : lo + P])

        def v_tile_tanh(g, m, cb):
            vTs[(g, m)] = work.tile([P, GROUP], BF16, name="vT", tag="vT", bufs=8)
            column_tanh(vTs[(g, m)], cb, 3 + m)

        def v_tile(g, m):
            cb = bank([P, GROUP], F32, "cb")
            for a in range(column_pieces(g)):
                v_tile_passes(g, m, a, cb)
            v_tile_tanh(g, m, cb)

        def z_tile(g):
            zb = bank([P, GROUP], F32, "zb")
            for a in range(column_pieces(g)):
                column_passes(g, a, zb, wxq, wxsc)
            zts[g] = work.tile([P, GROUP], F32, name="zt", tag="zt")
            column_tanh(zts[g], zb, 0)
            kTs[g] = work.tile([P, GROUP], BF16, name="kT", tag="kT")
            nc.gpsimd.tensor_scalar(
                out=kTs[g][:],
                in0=zts[g][:],
                scalar1=columns_bias[:, 1:2],
                scalar2=columns_bias[:, 2:3],
                op0=ALU.mult,
                op1=ALU.add,
            )

        def turn(dst, src):
            words = src[:].bitcast(F32)
            for a in range(2):
                nc.tensor.transpose(dst[:, a, :], words[:, a * P : (a + 1) * P], ident[:])

        def turn_k(g):
            kt = bank([P, 2, S], F32, "kt")
            turn(kt, kTs[g])
            return kt

        def turn_v(g):
            cts = []
            for q in range(TURNED[g]):
                ct = bank([P, 2, 2, P], F32, "ct")
                for m in range(2):
                    turn(ct[:, m, :, :], vTs[(g, 2 * q + m)])
                cts.append(ct)
            return cts

        def k_copy(g, kt, copy):
            gks[g] = work.tile([P, S, 4], BF16, name="gk", tag="gk", align_bytes=64)
            words = gks[g][:].rearrange("p s j -> p (s j)").bitcast(F32)
            copy(out=words.rearrange("p (s a) -> p s a", a=2), in_=kt[:].rearrange("p a s -> p s a"))

        def v_copy(g, q, ct, copy):
            words = gvs[g][:].rearrange("p e j -> p (e j)").bitcast(F32)[:, 2 * q * EQ : 2 * (q + 1) * EQ]
            copy(out=words.rearrange("p (m e a) -> p m e a", m=2, a=2), in_=ct[:].rearrange("p m a e -> p m e a"))

        def quant_v(g, lo, hi):
            nc.vector.quantize_mx(
                out=vqs[g][:, lo:hi].bitcast(FP8X4),
                scales=vscs[g][:, lo:hi],
                in_=gvs[g][:, lo:hi, :].rearrange("p e j -> p (e j)"),
            )

        def quant_k(g):
            kqs[g] = const.tile([P, S], U32, name="kq%d" % g, align_bytes=256)
            kscs[g] = const.tile([P, S], U8, name="ksc%d" % g, align_bytes=256)
            nc.vector.quantize_mx(
                out=kqs[g][:].bitcast(FP8X4), scales=kscs[g][:], in_=gks[g][:].rearrange("p s j -> p (s j)")
            )

        def kv_pass(kv, g, lo, hi):
            nc.tensor.matmul_mx(
                out=kv[:],
                lhsT=kqs[g][:].bitcast(FP8X4),
                lhsT_scale=kscs[g][:],
                rhs=vqs[g][:, lo:hi].bitcast(FP8X4),
                rhs_scale=vscs[g][:, lo:hi],
                start=(g % GPB == 0),
                stop=(g % GPB == GPB - 1),
            )

        def kv_store(b, lo, hi, kv, copy):
            row = work.tile([P, hi - lo], F32, name="row", tag="row", bufs=6)
            copy(out=row[:], in_=kv[:])
            nc.sync.dma_start(out=out[b, :, lo:hi], in_=row[:])

        def first_sum(q):
            kv = bank([P, EQ], F32, "kv")
            for g in range(GPB):
                kv_pass(kv, g, q * EQ, (q + 1) * EQ)
            return kv

        regroup_w(on_v, 0, 0)
        regroup_w(on_s, 1, 0)
        regroup_w(on_v, 0, 1)
        regroup_w(on_s, 1, 1)
        quant_w(0)
        new_v(0)
        xts = [x_transposes(0, 0)]
        keep_clock(1)
        xts.append(x_transposes(0, 1))
        keep_clock(2)
        x_copy(0, 0, xts[0], on_v)
        x_copy(0, 1, xts[1], on_s)
        quant_w(1)
        quant_x(0, 0)
        xts = [x_transposes(0, j) for j in range(2, 4)]
        cols = bank([P, 3 + MAX_TURNED], F32, "cols")
        for i in range(3 + MAX_TURNED):
            lo = E + i * S if i < 3 else (i - 3) * P
            nc.tensor.matmul(out=cols[:, i : i + 1], lhsT=rows[:, lo : lo + P], rhs=ones[:, 0:1], start=True, stop=True)
        bias = const.tile([P, E], BF16, name="bias")
        bb = bank([P, E], BF16, "bb")
        for h in range(2):
            cut = slice(h * 512, (h + 1) * 512)
            nc.tensor.matmul(out=bb[:, cut], lhsT=ones[:, 0:P], rhs=rows[:, cut], start=True, stop=True)
        x_copy(0, 2, xts[0], on_s)
        x_copy(0, 3, xts[1], on_v)
        for c in range(2):
            regroup(on_v, wxg[:, c, :, :], wxraw[:, c, :, :])
        quant_x(0, 1)
        on_s(out=bias[:], in_=bb[:])
        vbs = [quarter_half_passes(0, 1, 0)]
        cbs = [bank([P, GROUP], F32, "cb") for m in range(2)]
        for a in range(2):
            for m in range(2):
                v_tile_passes(0, m, a, cbs[m])
        columns_bias = const.tile([P, 3 + MAX_TURNED], F32, name="columns_bias")
        on_v(out=columns_bias[:], in_=cols[:])
        quant_wx()
        for c in range(2):
            regroup_w(on_v, 2, c)
            regroup_w(on_s, 3, c)
        vbs.append(quarter_half_passes(0, 1, 1))
        quarter_half_add(0, 1, 0, vbs[0])
        quant_w(2)
        for m in range(2):
            v_tile_tanh(0, m, cbs[m])
        z_tile(0)
        quarter_half_add(0, 1, 1, vbs[1])
        quant_w(3)
        xts = [x_transposes(1, j) for j in range(2)]
        quarter_half(0, 2, 0)
        x_copy(1, 0, xts[0], on_s)
        x_copy(1, 1, xts[1], on_v)
        quarter_tanh(0, 1)
        quarter_half(0, 2, 1)
        xts = [x_transposes(1, j) for j in range(2, 4)]
        x_copy(1, 2, xts[0], on_s)
        quant_x(1, 0)
        x_copy(1, 3, xts[1], on_s)
        quarter_half(0, 3, 0)
        quarter_tanh(0, 2)
        quant_x(1, 1)
        xts = [x_transposes(2, j) for j in range(2)]
        x_copy(2, 0, xts[0], on_v)
        x_copy(2, 1, xts[1], on_s)
        quarter_half(0, 3, 1)
        load_x_blocks(4)

        for g in range(1, FIRST_BLOCKED - 1):
            xts = [x_transposes(g + 1, j) for j in range(2, 4)]
            kt = turn_k(g - 1)
            cts = turn_v(g - 1)
            x_copy(g + 1, 2, xts[0], on_s)
            quarter_tanh(g - 1, 3)
            x_copy(g + 1, 3, xts[1], on_s)
            v_copy(g - 1, 0, cts[0], on_v)
            k_copy(g - 1, kt, on_s)
            new_v(g)
            quarter_half(g, 1, 0)
            quant_x(g + 1, 0)
            z_tile(g)
            quarter_half(g, 1, 1)
            quarter_tanh(g, 1)
            quant_v(g - 1, 0, 512)
            if g + 2 == FIRST_BLOCKED:
                x_blocks(g + 2, 0)
            v_tile(g, 0)
            quarter_half(g, 2, 0)
            if g + 2 < FIRST_BLOCKED:
                xts = [x_transposes(g + 2, j) for j in range(2)]
                for j in range(2):
                    x_copy(g + 2, j, xts[j], on_s)
            quant_k(g - 1)
            quant_x(g + 1, 1)
            v_tile(g, 1)
            quarter_half(g, 2, 1)
            quarter_tanh(g, 2)
            quarter_half(g, 3, 0)
            quarter_half(g, 3, 1)
            quant_v(g - 1, 512, 1024)
            load_x_blocks(g + 4)

        def open_step(g, copies):
            quarter_tanh(g - 1, 3)
            x_blocks(g + 1, 1)
            new_v(g)
            z_tile(g)
            v_tile(g, 0)
            quarter_half(g, TURNED[g], 0)
            kt = turn_k(g - 1)
            cts = turn_v(g - 1)
            k_copy(g - 1, kt, on_s)
            for q, ct in enumerate(cts):
                v_copy(g - 1, q, ct, copies[q])
            quant_x(g + 1, 0)
            v_tile(g, 1)

        for g in range(FIRST_BLOCKED - 1, NG - 2):
            open_step(g, [on_v, on_s, on_s])
            v_tile(g, 2)
            quant_x(g + 1, 1)
            quarter_half(g, 3, 1)
            quant_v(g - 1, 512, 1024)
            v_tile(g, 3)
            quant_v(g - 1, 0, 512)
            quant_k(g - 1)
            if g > GPB:
                kv_store(0, 0, EQ, first_sum(0), on_s)
            v_tile(g, 4)
            x_blocks(g + 2, 0)
            v_tile(g, 5)
            if g + 4 < NG:
                load_x_blocks(g + 4)
        g = NG - 2
        open_step(g, [on_s, on_s, on_s])
        quarter_half(g, 2, 1)
        quarter_tanh(g, 2)
        v_tile(g, 2)
        quant_x(g + 1, 1)
        quant_v(g - 1, 512, 1024)
        quarter_half(g, 3, 0)
        quant_v(g - 1, 0, 512)
        quant_k(g - 1)
        kv_store(0, EQ, 2 * EQ, first_sum(1), on_s)
        v_tile(g, 3)
        quarter_half(g, 3, 1)

        g = NG - 1
        new_v(g)
        quarter_half(g, 0, 0)
        z_tile(g)
        quarter_tanh(g - 1, 3)
        quarter_half(g, 0, 1)
        kt = turn_k(g - 1)
        cts = turn_v(g - 1)
        k_copy(g - 1, kt, on_s)
        v_copy(g - 1, 0, cts[0], on_v)
        v_copy(g - 1, 1, cts[1], on_s)
        quarter_half(g, 1, 0)
        quarter_tanh(g, 0)
        quarter_half(g, 1, 1)
        quant_v(g - 1, 0, 512)
        quarter_half(g, 2, 0)
        quarter_tanh(g, 1)
        kt = turn_k(g)
        k_copy(g, kt, on_s)
        quarter_half(g, 2, 1)
        quant_k(g - 1)
        quant_v(g - 1, 512, 1024)
        quarter_tanh(g, 2)
        eighth(g, 3 * EQ)
        eighth(g, 3 * EQ + P)
        rest_of_first = [(q, first_sum(q)) for q in (2, 3)]
        quant_k(g)
        cuts = [(0, 512), (512, 768), (768, 896), (896, 1024)]
        kvs = [bank([P, hi - lo], F32, "kv") for lo, hi in cuts]
        for kv, (lo, hi) in zip(kvs, cuts):
            for gg in range(GPB, g):
                kv_pass(kv, gg, lo, hi)
        for kv, (lo, hi) in zip(kvs, cuts):
            quant_v(g, lo, hi)
            kv_pass(kv, g, lo, hi)
        for q, kv in rest_of_first:
            kv_store(0, q * EQ, (q + 1) * EQ, kv, on_s)
        for i, (kv, (lo, hi)) in enumerate(zip(kvs, cuts)):
            kv_store(1, lo, hi, kv, on_v if i % 2 == 0 else on_s)
